import numpy as np
import ml_dtypes


def mxq(x, axis, fmt="e4m3"):
    dtype, down = {"e4m3": (ml_dtypes.float8_e4m3fn, 7), "e5m2": (ml_dtypes.float8_e5m2, 14)}[fmt]
    v = np.moveaxis(np.asarray(x, np.float32).astype(ml_dtypes.bfloat16).astype(np.float64), axis, -1)
    blocks = v.reshape(v.shape[:-1] + (-1, 32))
    amax = np.abs(blocks).max(-1, keepdims=True)
    byte = np.maximum(np.where(amax > 0, np.frexp(amax)[1] - 1 + 127, 0) - down, 1)
    scale = np.exp2(byte - 127.0)
    codes = (blocks / scale).astype(np.float32).astype(dtype).astype(np.float64)
    return np.moveaxis((codes * scale).reshape(v.shape), -1, axis)


WIDE = False


def mx_kscale(k):
    if not WIDE:
        return np.ones(k)
    levels = np.array([10, -10, 5, -5, 0])
    a = np.random.permutation(np.resize(levels, k // 512 * 4)).reshape(k // 512, 4)
    idx = np.arange(k)
    return np.exp2(a[idx // 512, idx % 128 // 32])


BF16 = ml_dtypes.bfloat16


def bf(x):
    return np.asarray(x, np.float32).astype(BF16)


def f64(x):
    return np.asarray(x).astype(np.float64)


B, C, H, L = 2, 512, 512, 1024


def sigmoid(v):
    return 1.0 / (1.0 + np.exp(-v))


def pconv(xq, W, b):
    return (mxq(f64(W), 1, "e4m3") @ xq) + f64(b)[None, :, None]


def setup_inputs():
    s = np.concatenate([mx_kscale(C + H)[:C], np.ones(H)])
    w = lambda: bf(np.random.standard_normal((H, C + H)) / np.sqrt(C + H) / s)
    b = lambda: bf(np.random.standard_normal(H) * 0.3)
    return {"input": bf(np.random.standard_normal((B, C, L)) * s[:C, None]), "h": bf(np.random.standard_normal((B, H, L))),
            "W_r": w(), "b_r": b(), "W_u": w(), "b_u": b(), "W_h": w(), "b_h": b()}


def reference(input, h, W_r, b_r, W_u, b_u, W_h, b_h):
    h = f64(h)
    xq = mxq(f64(input), 1, "e4m3")
    input_h = np.concatenate([xq, mxq(h, 1, "e4m3")], axis=1)
    reset_h = sigmoid(pconv(input_h, W_r, b_r))
    update_h = sigmoid(pconv(input_h, W_u, b_u))
    input_new_h = np.concatenate([xq, mxq(h * reset_h, 1, "e4m3")], axis=1)
    new_h = np.tanh(pconv(input_new_h, W_h, b_h))
    return (1.0 - update_h) * new_h + update_h * h

@@ -1,0 +1,492 @@
+from contextlib import ExitStack
+
+import concourse.mybir as mybir
+from concourse.masks import make_identity
+
+F32 = mybir.dt.float32
+BF16 = mybir.dt.bfloat16
+U32 = mybir.dt.uint32
+U8 = mybir.dt.uint8
+FP8X4 = mybir.dt.float8_e4m3fn_x4
+ACT = mybir.ActivationFunctionType
+ALU = mybir.AluOpType
+
+P = 128
+T = 4
+B = 2
+CH = 512
+L = 1024
+FLOPS = 2 * 3 * CH * (2 * CH) * B * L
+PIN = True
+CHUNKS = ((0, 0, 512), (0, 512, 512), (1, 0, 512), (1, 512, 512))
+PLAN = [
+    ("LD", "w", 0, 0),
+    ("LD", "w", 0, 1),
+    ("LD", "w", 1, 0),
+    ("LD", "w", 1, 1),
+    ("LD", "h", 0, 0),
+    ("LD", "h", 0, 1),
+    ("LD", "x", 1, 0),
+    ("LD", "x", 1, 1),
+    ("LD", "x", 0, 0),
+    ("LD", "x", 0, 1),
+    ("LD", "w", 2, 0),
+    ("LD", "w", 2, 1),
+    ("LD", "h", 2, 0),
+    ("LD", "h", 2, 1),
+    ("LD", "h", 1, 0),
+    ("LD", "h", 1, 1),
+    ("LD", "x", 2, 0),
+    ("LD", "x", 2, 1),
+    ("LD", "h", 3, 0),
+    ("LD", "h", 3, 1),
+    ("LD", "x", 3, 0),
+    ("LD", "x", 3, 1),
+    ("WT", 0, 1),
+    ("WT", 0, 2),
+    ("WT", 0, 3),
+    ("WC", 0, 3, "S"),
+    ("WT", 1, 0),
+    ("WC", 0, 2, "S"),
+    ("WQ", 0, (2,)),
+    ("WT", 1, 1),
+    ("WC", 1, 1, "S"),
+    ("G", "h", 0, "V"),
+    ("WT", 1, 2),
+    ("WC", 0, 1, "S"),
+    ("WT", 0, 0),
+    ("WC", 1, 2, "S"),
+    ("WT", 1, 3),
+    ("WC", 0, 0, "S"),
+    ("WQ", 0, (0,)),
+    ("WT", 2, 0),
+    ("WC", 1, 3, "S"),
+    ("WQ", 0, (1,)),
+    ("WT", 2, 1),
+    ("WC", 1, 0, "S"),
+    ("Q", "h", 0),
+    ("WT", 2, 2),
+    ("G", "x", 1, "S"),
+    ("WQ", 1, (1,)),
+    ("WC", 2, 0, "S"),
+    ("WQ", 1, (0,)),
+    ("WC", 2, 1, "S"),
+    ("WQ", 0, (3,)),
+    ("WC", 2, 2, "S"),
+    ("G", "x", 0, "V"),
+    ("Q", "x", 0),
+    ("MM1", 0, 0, 0),
+    ("WQ", 1, (3,)),
+    ("MM2", 0, 0, 0),
+    ("ACT", 0, 0, 0),
+    ("WQ", 2, (0,)),
+    ("MM1", 0, 0, 1),
+    ("WQ", 2, (1,)),
+    ("MM2", 0, 0, 1),
+    ("ACT", 0, 0, 1),
+    ("WQ", 1, (2,)),
+    ("MM1", 0, 0, 2),
+    ("WQ", 2, (2,)),
+    ("MM2", 0, 0, 2),
+    ("ACT", 0, 0, 2),
+    ("G", "h", 2, "V"),
+    ("MM1", 0, 0, 3),
+    ("Q", "h", 2),
+    ("MM2", 0, 0, 3),
+    ("ACT", 0, 0, 3),
+    ("G", "h", 1, "V"),
+    ("MM1", 1, 0, 0),
+    ("V1", 0),
+    ("MM2", 1, 0, 0),
+    ("ACT", 1, 0, 0),
+    ("Q", "hr", 0),
+    ("MM1", 1, 0, 1),
+    ("MM2", 1, 0, 1),
+    ("ACT", 1, 0, 1),
+    ("MM1", 1, 0, 2),
+    ("MM2", 1, 0, 2),
+    ("ACT", 1, 0, 2),
+    ("MM1", 1, 0, 3),
+    ("MM2", 1, 0, 3),
+    ("ACT", 1, 0, 3),
+    ("WT", 2, 3),
+    ("WC", 2, 3, "S"),
+    ("WQ", 2, (3,)),
+    ("MM1", 2, 0, 0),
+    ("G", "x", 2, "S"),
+    ("Q", "x", 1),
+    ("MM2", 2, 0, 0),
+    ("ACT", 2, 0, 0),
+    ("Q", "h", 1),
+    ("MM1", 2, 0, 1),
+    ("A", 0),
+    ("MM2", 2, 0, 1),
+    ("ACT", 2, 0, 1),
+    ("MM1", 2, 0, 2),
+    ("MM2", 2, 0, 2),
+    ("ACT", 2, 0, 2),
+    ("MM1", 2, 0, 3),
+    ("MM2", 2, 0, 3),
+    ("ACT", 2, 0, 3),
+    ("B", 0, (0, 1, 2, 3)),
+    ("MM1", 0, 1, 0),
+    ("MM2", 0, 1, 0),
+    ("ACT", 0, 1, 0),
+    ("MM1", 0, 1, 1),
+    ("MM2", 0, 1, 1),
+    ("ACT", 0, 1, 1),
+    ("MM1", 0, 1, 2),
+    ("MM2", 0, 1, 2),
+    ("ACT", 0, 1, 2),
+    ("MM1", 0, 1, 3),
+    ("MM2", 0, 1, 3),
+    ("ACT", 0, 1, 3),
+    ("V1", 1),
+    ("MM1", 1, 1, 0),
+    ("Q", "hr", 1),
+    ("MM2", 1, 1, 0),
+    ("ACT", 1, 1, 0),
+    ("O", 0, (0, 1, 2, 3)),
+    ("ST", 0, (0, 1)),
+    ("ST", 0, (2, 3)),
+    ("MM1", 1, 1, 1),
+    ("Q", "x", 2),
+    ("MM2", 1, 1, 1),
+    ("ACT", 1, 1, 1),
+    ("MM1", 1, 1, 2),
+    ("MM2", 1, 1, 2),
+    ("ACT", 1, 1, 2),
+    ("MM1", 1, 1, 3),
+    ("MM2", 1, 1, 3),
+    ("ACT", 1, 1, 3),
+    ("A", 1),
+    ("MM1", 2, 1, 0),
+    ("G", "h", 3, "S"),
+    ("MM2", 2, 1, 0),
+    ("ACT", 2, 1, 0),
+    ("MM1", 2, 1, 1),
+    ("MM2", 2, 1, 1),
+    ("ACT", 2, 1, 1),
+    ("MM1", 2, 1, 2),
+    ("MM2", 2, 1, 2),
+    ("ACT", 2, 1, 2),
+    ("MM1", 2, 1, 3),
+    ("MM2", 2, 1, 3),
+    ("ACT", 2, 1, 3),
+    ("B", 1, (0, 1, 2, 3)),
+    ("MM1", 0, 2, 0),
+    ("MM2", 0, 2, 0),
+    ("ACT", 0, 2, 0),
+    ("MM1", 0, 2, 1),
+    ("MM2", 0, 2, 1),
+    ("ACT", 0, 2, 1),
+    ("MM1", 0, 2, 2),
+    ("MM2", 0, 2, 2),
+    ("ACT", 0, 2, 2),
+    ("MM1", 0, 2, 3),
+    ("MM2", 0, 2, 3),
+    ("ACT", 0, 2, 3),
+    ("V1", 2),
+    ("MM1", 1, 2, 0),
+    ("G", "x", 3, "S"),
+    ("Q", "hr", 2),
+    ("MM2", 1, 2, 0),
+    ("ACT", 1, 2, 0),
+    ("Q", "h", 3),
+    ("MM1", 1, 2, 1),
+    ("Q", "x", 3),
+    ("MM2", 1, 2, 1),
+    ("ACT", 1, 2, 1),
+    ("MM1", 1, 2, 2),
+    ("MM2", 1, 2, 2),
+    ("ACT", 1, 2, 2),
+    ("MM1", 1, 2, 3),
+    ("MM2", 1, 2, 3),
+    ("ACT", 1, 2, 3),
+    ("A", 2),
+    ("MM1", 2, 2, 0),
+    ("O", 1, (0, 1, 2, 3)),
+    ("ST", 1, (0, 1)),
+    ("ST", 1, (2, 3)),
+    ("MM2", 2, 2, 0),
+    ("ACT", 2, 2, 0),
+    ("MM1", 2, 2, 1),
+    ("MM2", 2, 2, 1),
+    ("ACT", 2, 2, 1),
+    ("MM1", 2, 2, 2),
+    ("MM2", 2, 2, 2),
+    ("ACT", 2, 2, 2),
+    ("MM1", 2, 2, 3),
+    ("MM2", 2, 2, 3),
+    ("ACT", 2, 2, 3),
+    ("MM1", 0, 3, 0),
+    ("MM2", 0, 3, 0),
+    ("ACT", 0, 3, 0),
+    ("MM1", 0, 3, 1),
+    ("MM2", 0, 3, 1),
+    ("ACT", 0, 3, 1),
+    ("MM1", 0, 3, 2),
+    ("MM2", 0, 3, 2),
+    ("ACT", 0, 3, 2),
+    ("MM1", 0, 3, 3),
+    ("MM2", 0, 3, 3),
+    ("ACT", 0, 3, 3),
+    ("V1", 3),
+    ("MM1", 1, 3, 0),
+    ("Q", "hr", 3),
+    ("MM2", 1, 3, 0),
+    ("ACT", 1, 3, 0),
+    ("MM1", 1, 3, 1),
+    ("MM2", 1, 3, 1),
+    ("ACT", 1, 3, 1),
+    ("MM1", 1, 3, 2),
+    ("MM2", 1, 3, 2),
+    ("ACT", 1, 3, 2),
+    ("MM1", 1, 3, 3),
+    ("MM2", 1, 3, 3),
+    ("ACT", 1, 3, 3),
+    ("A", 3),
+    ("MM1", 2, 3, 0),
+    ("B", 2, (0, 1, 2, 3)),
+    ("MM2", 2, 3, 0),
+    ("ACT", 2, 3, 0),
+    ("O", 2, (0, 1, 2, 3)),
+    ("ST", 2, (0, 1)),
+    ("ST", 2, (2, 3)),
+    ("MM1", 2, 3, 1),
+    ("B", 3, (0,)),
+    ("MM2", 2, 3, 1),
+    ("ACT", 2, 3, 1),
+    ("O", 3, (0,)),
+    ("ST", 3, (0,)),
+    ("MM1", 2, 3, 2),
+    ("B", 3, (1,)),
+    ("MM2", 2, 3, 2),
+    ("ACT", 2, 3, 2),
+    ("O", 3, (1,)),
+    ("ST", 3, (1,)),
+    ("MM1", 2, 3, 3),
+    ("B", 3, (2,)),
+    ("MM2", 2, 3, 3),
+    ("ACT", 2, 3, 3),
+    ("O", 3, (2,)),
+    ("ST", 3, (2,)),
+    ("B", 3, (3,)),
+    ("O", 3, (3,)),
+    ("ST", 3, (3,)),
+]
+
+
+def tile_gru_kernel(tc, x, h, w_r, b_r, w_u, b_u, w_h, b_h, out):
+    nc = tc.nc
+    weights = [w_r, w_u, w_h]
+    biases = [b_r, b_u, b_h]
+    funcs = [ACT.Sigmoid, ACT.Sigmoid, ACT.Tanh]
+    with ExitStack() as ctx:
+        keep = ctx.enter_context(tc.tile_pool(name="keep", bufs=1))
+        rot = ctx.enter_context(tc.tile_pool(name="rot", bufs=2))
+        psum = ctx.enter_context(tc.psum_pool(name="psum", bufs=8))
+
+        warm = keep.tile([P, 1], F32, name="warm")
+        warm_out = keep.tile([P, 1], F32, name="warm_out")
+        nc.vector.memset(warm[:], 0.0)
+        nc.scalar.activation(out=warm_out[:], in_=warm[:], func=ACT.Sigmoid)
+        ident = keep.tile([P, P], F32, name="ident")
+        make_identity(nc, ident[:])
+
+        raw = {}
+        for nm in ("x", "h"):
+            for b in range(B):
+                raw[(nm, b)] = keep.tile([P, T, L], BF16, name="raw_%s%d" % (nm, b))
+        dram = {"x": x, "h": h}
+        w_sb = [keep.tile([P, T, 2 * CH], BF16, name="w_sb%d" % g) for g in range(3)]
+        wq = [keep.tile([P, T * 2 * P], U32, name="wq%d" % g, align_bytes=64) for g in range(3)]
+        ws = [keep.tile([P, T * 2 * P], U8, name="ws%d" % g, align_bytes=64) for g in range(3)]
+        codes = {}
+        scales = {}
+        for nm in ("x", "h", "hr"):
+            codes[nm] = keep.tile([P, B * L], U32, name="codes_%s" % nm, align_bytes=64)
+            scales[nm] = keep.tile([P, B * L], U8, name="scales_%s" % nm, align_bytes=64)
+        bias_bf = [keep.tile([P, T], BF16, name="bias_bf%d" % g) for g in range(3)]
+        bias = [keep.tile([P, T], F32, name="bias%d" % g) for g in range(3)]
+
+        def rows(ap2d):
+            return ap2d.rearrange("(u p e) l -> p u e l", u=2, p=P, e=2)
+
+        for g in range(3):
+            nc.scalar.dma_start(
+                out=bias_bf[g][:].rearrange("p (u e) -> p u e", u=2),
+                in_=biases[g].rearrange("(u p e) -> p u e", u=2, p=P, e=2),
+            )
+        for g in range(3):
+            nc.vector.tensor_copy(out=bias[g][:], in_=bias_bf[g][:])
+
+        grp = {}
+        w_grp = {}
+        bank = {}
+        gate = {}
+        mix = {}
+
+        def gcol(c):
+            b, lo, w = CHUNKS[c]
+            return b * L + lo
+
+        def do_ld(kind, a, u):
+            if kind == "w":
+                nc.sync.dma_start(out=w_sb[a][:, 2 * u : 2 * u + 2, :], in_=rows(weights[a])[:, u, :, :])
+            else:
+                b, lo, w = CHUNKS[a]
+                nc.sync.dma_start(
+                    out=raw[(kind, b)][:, 2 * u : 2 * u + 2, lo : lo + w], in_=rows(dram[kind][b])[:, u, :, lo : lo + w]
+                )
+
+        def do_g(nm, c, e):
+            b, lo, w = CHUNKS[c]
+            if nm == "x":
+                dst = rot.tile([P, w, T], BF16, name="x_grp", tag="x_grp", bufs=2, align_bytes=64)
+            else:
+                dst = keep.tile([P, w, T], BF16, name="h_grp%d" % c, align_bytes=64)
+            grp[(nm, c)] = dst
+            o_ap = dst[:].rearrange("p (c i) t -> p c t i", i=4)
+            i_ap = raw[(nm, b)][:, :, lo : lo + w].rearrange("p t (c i) -> p c t i", i=4)
+            if e == "V":
+                nc.vector.tensor_copy(out=o_ap, in_=i_ap)
+            else:
+                nc.scalar.copy(out=o_ap, in_=i_ap)
+
+        def do_q(nm, c):
+            b, lo, w = CHUNKS[c]
+            g0 = gcol(c)
+            nc.vector.quantize_mx(
+                out=codes[nm][:, g0 : g0 + w].bitcast(FP8X4),
+                scales=scales[nm][:, g0 : g0 + w],
+                in_=grp[(nm, c)][:].rearrange("p l t -> p (l t)"),
+            )
+
+        def do_wt(g, t):
+            w32 = w_sb[g][:].bitcast(F32)
+            bk = psum.tile([P, 4, P], F32, name="bank", tag="bank")
+            bank[("w", g, t)] = bk
+            for a in range(4):
+                nc.tensor.transpose(bk[:, a, :], w32[:, t, a * P : (a + 1) * P], ident[:])
+
+        def do_wc(g, t, e):
+            if g not in w_grp:
+                w_grp[g] = rot.tile([P, T * 2 * P * 4], BF16, name="w_grp", tag="w_grp", bufs=2, align_bytes=64)
+            g32 = w_grp[g][:].bitcast(F32).rearrange("p (t g o u) -> p t g o u", t=T, g=2, o=P, u=2)
+            src = bank[("w", g, t)][:].rearrange("p (g u) o -> p g o u", g=2)
+            if e == "V":
+                nc.vector.tensor_copy(out=g32[:, t], in_=src)
+            else:
+                nc.scalar.copy(out=g32[:, t], in_=src)
+
+        def do_wq(g, ts):
+            t0 = ts[0]
+            n = len(ts)
+            nc.vector.quantize_mx(
+                out=wq[g][:, t0 * 2 * P : (t0 + n) * 2 * P].bitcast(FP8X4),
+                scales=ws[g][:, t0 * 2 * P : (t0 + n) * 2 * P],
+                in_=w_grp[g][:, t0 * 8 * P : (t0 + n) * 8 * P],
+            )
+
+        def do_mm(g, c, t, k):
+            b, lo, w = CHUNKS[c]
+            g0 = gcol(c)
+            if k == 0:
+                bank[(g, c, t)] = psum.tile([P, 512], F32, name="bank", tag="bank")
+            nm = "x" if k == 0 else ("hr" if g == 2 else "h")
+            wsl = slice((t * 2 + k) * P, (t * 2 + k + 1) * P)
+            nc.tensor.matmul_mx(
+                out=bank[(g, c, t)][:, 0:w],
+                lhsT=wq[g][:, wsl].bitcast(FP8X4),
+                lhsT_scale=ws[g][:, wsl],
+                rhs=codes[nm][:, g0 : g0 + w].bitcast(FP8X4),
+                rhs_scale=scales[nm][:, g0 : g0 + w],
+                start=(k == 0),
+                stop=(k == 1),
+            )
+
+        def do_act(g, c, t):
+            b, lo, w = CHUNKS[c]
+            if (g, c) not in gate:
+                nm = ("r_sb", "u_sb", "n_sb")[g]
+                gate[(g, c)] = rot.tile([P, T, w], F32, name=nm, tag=nm, bufs=(2, 2, 2)[g])
+            nc.scalar.activation(
+                out=gate[(g, c)][:, t, :], in_=bank[(g, c, t)][:, 0:w], func=funcs[g], bias=bias[g][:, t : t + 1], scale=1.0
+            )
+
+        def do_v1(c):
+            b, lo, w = CHUNKS[c]
+            dst = rot.tile([P, w, T], BF16, name="hr_grp", tag="hr_grp", bufs=2, align_bytes=64)
+            grp[("hr", c)] = dst
+            nc.vector.tensor_tensor(
+                out=dst[:], in0=grp[("h", c)][:], in1=gate[(0, c)][:].rearrange("p t l -> p l t"), op=ALU.mult
+            )
+
+        def do_a(c):
+            b, lo, w = CHUNKS[c]
+            mix[c] = rot.tile([P, T, w], F32, name="a_sb", tag="a_sb", bufs=3)
+            nc.vector.tensor_tensor(out=mix[c][:], in0=gate[(1, c)][:], in1=raw[("h", b)][:, :, lo : lo + w], op=ALU.mult)
+
+        def flat(ap, ts):
+            return ap[:, ts[0] : ts[0] + len(ts), :].rearrange("p t l -> p (t l)")
+
+        def do_b(c, ts):
+            nf = flat(gate[(2, c)], ts)
+            nc.vector.scalar_tensor_tensor(
+                out=nf, in0=flat(gate[(1, c)], ts), scalar=1.0, in1=nf, op0=ALU.subtract, op1=ALU.mult
+            )
+
+        def do_o(c, ts):
+            af = flat(mix[c], ts)
+            nc.vector.tensor_tensor(out=af, in0=af, in1=flat(gate[(2, c)], ts), op=ALU.subtract)
+
+        def do_st(c, ts):
+            b, lo, w = CHUNKS[c]
+            view = rows(out[b])
+            if len(ts) == 2:
+                u = ts[0] // 2
+                nc.sync.dma_start(out=view[:, u, :, lo : lo + w], in_=mix[c][:, 2 * u : 2 * u + 2, :])
+            else:
+                t = ts[0]
+                nc.sync.dma_start(out=view[:, t // 2, t % 2, lo : lo + w], in_=mix[c][:, t, :])
+
+        def run_plan():
+            for op in PLAN:
+                k = op[0]
+                if k == "LD":
+                    do_ld(op[1], op[2], op[3])
+                elif k == "G":
+                    do_g(op[1], op[2], op[3])
+                elif k == "Q":
+                    do_q(op[1], op[2])
+                elif k == "WT":
+                    do_wt(op[1], op[2])
+                elif k == "WC":
+                    do_wc(op[1], op[2], op[3])
+                elif k == "WQ":
+                    do_wq(op[1], op[2])
+                elif k == "MM1":
+                    do_mm(op[1], op[2], op[3], 0)
+                elif k == "MM2":
+                    do_mm(op[1], op[2], op[3], 1)
+                elif k == "ACT":
+                    do_act(op[1], op[2], op[3])
+                elif k == "V1":
+                    do_v1(op[1])
+                elif k == "A":
+                    do_a(op[1])
+                elif k == "B":
+                    do_b(op[1], op[2])
+                elif k == "O":
+                    do_o(op[1], op[2])
+                elif k == "ST":
+                    do_st(op[1], op[2])
+                else:
+                    raise ValueError(k)
+
+        if PIN:
+            with tc.manual_schedule():
+                run_plan()
+        else:
+            run_plan()

@@ -20,86 +20,98 @@ FLOPS = 2 * 3 * CH * (2 * CH) * B * L
 PIN = True
 CHUNKS = ((0, 0, 512), (0, 512, 512), (1, 0, 512), (1, 512, 512))
 PLAN = [
-    ("LD", "w", 0, 0),
-    ("LD", "w", 0, 1),
-    ("LD", "w", 1, 0),
-    ("LD", "w", 1, 1),
-    ("LD", "h", 0, 0),
-    ("LD", "h", 0, 1),
-    ("LD", "x", 1, 0),
-    ("LD", "x", 1, 1),
     ("LD", "x", 0, 0),
     ("LD", "x", 0, 1),
-    ("LD", "w", 2, 0),
-    ("LD", "w", 2, 1),
-    ("LD", "h", 2, 0),
-    ("LD", "h", 2, 1),
+    ("LD", "h", 0, 0),
+    ("LD", "h", 0, 1),
+    ("LD", "w", 0, 0),
+    ("LD", "w", 0, 1),
+    ("LD", "x", 1, 0),
+    ("LD", "x", 1, 1),
     ("LD", "h", 1, 0),
     ("LD", "h", 1, 1),
+    ("LD", "w", 1, 0),
+    ("LD", "w", 1, 1),
+    ("LD", "w", 2, 0),
+    ("LD", "w", 2, 1),
     ("LD", "x", 2, 0),
     ("LD", "x", 2, 1),
-    ("LD", "h", 3, 0),
-    ("LD", "h", 3, 1),
+    ("LD", "h", 2, 0),
+    ("LD", "h", 2, 1),
     ("LD", "x", 3, 0),
     ("LD", "x", 3, 1),
-    ("WT", 0, 1),
-    ("WT", 0, 2),
-    ("WT", 0, 3),
-    ("WC", 0, 3, "S"),
-    ("WT", 1, 0),
-    ("WC", 0, 2, "S"),
-    ("WQ", 0, (2,)),
-    ("WT", 1, 1),
-    ("WC", 1, 1, "S"),
-    ("G", "h", 0, "V"),
-    ("WT", 1, 2),
-    ("WC", 0, 1, "S"),
+    ("LD", "h", 3, 0),
+    ("LD", "h", 3, 1),
     ("WT", 0, 0),
-    ("WC", 1, 2, "S"),
-    ("WT", 1, 3),
+    ("G", "x", 0, "S"),
+    ("G", "h", 0, "V"),
+    ("WT", 0, 1),
     ("WC", 0, 0, "S"),
-    ("WQ", 0, (0,)),
-    ("WT", 2, 0),
-    ("WC", 1, 3, "S"),
-    ("WQ", 0, (1,)),
-    ("WT", 2, 1),
-    ("WC", 1, 0, "S"),
-    ("Q", "h", 0),
-    ("WT", 2, 2),
-    ("G", "x", 1, "S"),
-    ("WQ", 1, (1,)),
-    ("WC", 2, 0, "S"),
-    ("WQ", 1, (0,)),
-    ("WC", 2, 1, "S"),
-    ("WQ", 0, (3,)),
-    ("WC", 2, 2, "S"),
-    ("G", "x", 0, "V"),
     ("Q", "x", 0),
+    ("WT", 0, 2),
+    ("WC", 0, 1, "S"),
+    ("Q", "h", 0),
+    ("WT", 0, 3),
+    ("WC", 0, 2, "S"),
+    ("WQ", 0, (0,)),
     ("MM1", 0, 0, 0),
-    ("WQ", 1, (3,)),
+    ("G", "x", 1, "S"),
+    ("WQ", 0, (1,)),
     ("MM2", 0, 0, 0),
     ("ACT", 0, 0, 0),
-    ("WQ", 2, (0,)),
+    ("WC", 0, 3, "V"),
     ("MM1", 0, 0, 1),
-    ("WQ", 2, (1,)),
+    ("WQ", 0, (2,)),
     ("MM2", 0, 0, 1),
     ("ACT", 0, 0, 1),
-    ("WQ", 1, (2,)),
+    ("WQ", 0, (3,)),
     ("MM1", 0, 0, 2),
-    ("WQ", 2, (2,)),
+    ("G", "h", 1, "V"),
     ("MM2", 0, 0, 2),
     ("ACT", 0, 0, 2),
-    ("G", "h", 2, "V"),
+    ("Q", "h", 1),
     ("MM1", 0, 0, 3),
-    ("Q", "h", 2),
+    ("Q", "x", 1),
     ("MM2", 0, 0, 3),
     ("ACT", 0, 0, 3),
-    ("G", "h", 1, "V"),
-    ("MM1", 1, 0, 0),
+    ("WT", 1, 0),
+    ("WC", 1, 0, "V"),
+    ("WT", 1, 1),
+    ("WC", 1, 1, "S"),
+    ("WQ", 1, (0,)),
+    ("WT", 1, 2),
+    ("WC", 1, 2, "S"),
     ("V1", 0),
+    ("WT", 1, 3),
+    ("WC", 1, 3, "S"),
+    ("WQ", 1, (1,)),
+    ("MM1", 0, 1, 0),
+    ("WQ", 1, (2,)),
+    ("WT", 2, 0),
+    ("WC", 2, 0, "S"),
+    ("WQ", 1, (3,)),
+    ("WT", 2, 1),
+    ("WC", 2, 1, "S"),
+    ("WQ", 2, (0,)),
+    ("MM2", 0, 1, 0),
+    ("WQ", 2, (1,)),
+    ("MM1", 1, 0, 0),
+    ("WT", 2, 2),
+    ("WC", 2, 2, "S"),
+    ("WQ", 2, (2,)),
+    ("WT", 2, 3),
+    ("WC", 2, 3, "S"),
+    ("WQ", 2, (3,)),
     ("MM2", 1, 0, 0),
     ("ACT", 1, 0, 0),
     ("Q", "hr", 0),
+    ("MM1", 0, 1, 1),
+    ("ACT", 0, 1, 0),
+    ("G", "x", 2, "V"),
+    ("MM2", 0, 1, 1),
+    ("Q", "x", 2),
+    ("MM1", 0, 1, 2),
+    ("MM2", 0, 1, 2),
     ("MM1", 1, 0, 1),
     ("MM2", 1, 0, 1),
     ("ACT", 1, 0, 1),
@@ -109,17 +121,18 @@ PLAN = [
     ("MM1", 1, 0, 3),
     ("MM2", 1, 0, 3),
     ("ACT", 1, 0, 3),
-    ("WT", 2, 3),
-    ("WC", 2, 3, "S"),
-    ("WQ", 2, (3,)),
+    ("A", 0),
+    ("MM1", 0, 1, 3),
+    ("ACT", 0, 1, 1),
+    ("MM2", 0, 1, 3),
+    ("ACT", 0, 1, 2),
     ("MM1", 2, 0, 0),
-    ("G", "x", 2, "S"),
-    ("Q", "x", 1),
+    ("ACT", 0, 1, 3),
+    ("V1", 1),
     ("MM2", 2, 0, 0),
     ("ACT", 2, 0, 0),
-    ("Q", "h", 1),
+    ("Q", "hr", 1),
     ("MM1", 2, 0, 1),
-    ("A", 0),
     ("MM2", 2, 0, 1),
     ("ACT", 2, 0, 1),
     ("MM1", 2, 0, 2),
@@ -129,28 +142,15 @@ PLAN = [
     ("MM2", 2, 0, 3),
     ("ACT", 2, 0, 3),
     ("B", 0, (0, 1, 2, 3)),
-    ("MM1", 0, 1, 0),
-    ("MM2", 0, 1, 0),
-    ("ACT", 0, 1, 0),
-    ("MM1", 0, 1, 1),
-    ("MM2", 0, 1, 1),
-    ("ACT", 0, 1, 1),
-    ("MM1", 0, 1, 2),
-    ("MM2", 0, 1, 2),
-    ("ACT", 0, 1, 2),
-    ("MM1", 0, 1, 3),
-    ("MM2", 0, 1, 3),
-    ("ACT", 0, 1, 3),
-    ("V1", 1),
     ("MM1", 1, 1, 0),
-    ("Q", "hr", 1),
+    ("G", "h", 2, "S"),
+    ("Q", "h", 2),
     ("MM2", 1, 1, 0),
     ("ACT", 1, 1, 0),
     ("O", 0, (0, 1, 2, 3)),
     ("ST", 0, (0, 1)),
     ("ST", 0, (2, 3)),
     ("MM1", 1, 1, 1),
-    ("Q", "x", 2),
     ("MM2", 1, 1, 1),
     ("ACT", 1, 1, 1),
     ("MM1", 1, 1, 2),
@@ -160,8 +160,11 @@ PLAN = [
     ("MM2", 1, 1, 3),
     ("ACT", 1, 1, 3),
     ("A", 1),
+    ("MM1", 0, 2, 0),
+    ("MM1", 0, 2, 1),
+    ("MM1", 0, 2, 2),
+    ("MM1", 0, 2, 3),
     ("MM1", 2, 1, 0),
-    ("G", "h", 3, "S"),
     ("MM2", 2, 1, 0),
     ("ACT", 2, 1, 0),
     ("MM1", 2, 1, 1),
@@ -172,32 +175,32 @@ PLAN = [
     ("ACT", 2, 1, 2),
     ("MM1", 2, 1, 3),
     ("MM2", 2, 1, 3),
-    ("ACT", 2, 1, 3),
-    ("B", 1, (0, 1, 2, 3)),
-    ("MM1", 0, 2, 0),
     ("MM2", 0, 2, 0),
     ("ACT", 0, 2, 0),
-    ("MM1", 0, 2, 1),
     ("MM2", 0, 2, 1),
     ("ACT", 0, 2, 1),
-    ("MM1", 0, 2, 2),
     ("MM2", 0, 2, 2),
     ("ACT", 0, 2, 2),
-    ("MM1", 0, 2, 3),
     ("MM2", 0, 2, 3),
     ("ACT", 0, 2, 3),
     ("V1", 2),
     ("MM1", 1, 2, 0),
-    ("G", "x", 3, "S"),
+    ("ACT", 2, 1, 3),
     ("Q", "hr", 2),
     ("MM2", 1, 2, 0),
+    ("G", "x", 3, "S"),
+    ("Q", "x", 3),
+    ("MM1", 1, 2, 1),
+    ("G", "h", 3, "S"),
+    ("B", 1, (0, 1, 2, 3)),
+    ("MM2", 1, 2, 1),
     ("ACT", 1, 2, 0),
     ("Q", "h", 3),
-    ("MM1", 1, 2, 1),
-    ("Q", "x", 3),
-    ("MM2", 1, 2, 1),
-    ("ACT", 1, 2, 1),
     ("MM1", 1, 2, 2),
+    ("ACT", 1, 2, 1),
+    ("O", 1, (0, 1, 2, 3)),
+    ("ST", 1, (0, 1)),
+    ("ST", 1, (2, 3)),
     ("MM2", 1, 2, 2),
     ("ACT", 1, 2, 2),
     ("MM1", 1, 2, 3),
@@ -205,38 +208,39 @@ PLAN = [
     ("ACT", 1, 2, 3),
     ("A", 2),
     ("MM1", 2, 2, 0),
-    ("O", 1, (0, 1, 2, 3)),
-    ("ST", 1, (0, 1)),
-    ("ST", 1, (2, 3)),
+    ("MM1", 2, 2, 1),
+    ("MM1", 2, 2, 2),
+    ("MM1", 2, 2, 3),
     ("MM2", 2, 2, 0),
     ("ACT", 2, 2, 0),
-    ("MM1", 2, 2, 1),
     ("MM2", 2, 2, 1),
     ("ACT", 2, 2, 1),
-    ("MM1", 2, 2, 2),
     ("MM2", 2, 2, 2),
-    ("ACT", 2, 2, 2),
-    ("MM1", 2, 2, 3),
     ("MM2", 2, 2, 3),
-    ("ACT", 2, 2, 3),
     ("MM1", 0, 3, 0),
+    ("MM1", 0, 3, 1),
+    ("MM1", 0, 3, 2),
+    ("MM1", 0, 3, 3),
     ("MM2", 0, 3, 0),
     ("ACT", 0, 3, 0),
-    ("MM1", 0, 3, 1),
     ("MM2", 0, 3, 1),
     ("ACT", 0, 3, 1),
-    ("MM1", 0, 3, 2),
     ("MM2", 0, 3, 2),
     ("ACT", 0, 3, 2),
-    ("MM1", 0, 3, 3),
     ("MM2", 0, 3, 3),
     ("ACT", 0, 3, 3),
     ("V1", 3),
     ("MM1", 1, 3, 0),
+    ("ACT", 2, 2, 2),
     ("Q", "hr", 3),
     ("MM2", 1, 3, 0),
-    ("ACT", 1, 3, 0),
+    ("ACT", 2, 2, 3),
+    ("B", 2, (0, 1, 2, 3)),
     ("MM1", 1, 3, 1),
+    ("ACT", 1, 3, 0),
+    ("O", 2, (0, 1, 2, 3)),
+    ("ST", 2, (0, 1)),
+    ("ST", 2, (2, 3)),
     ("MM2", 1, 3, 1),
     ("ACT", 1, 3, 1),
     ("MM1", 1, 3, 2),
@@ -247,28 +251,24 @@ PLAN = [
     ("ACT", 1, 3, 3),
     ("A", 3),
     ("MM1", 2, 3, 0),
-    ("B", 2, (0, 1, 2, 3)),
+    ("MM1", 2, 3, 1),
+    ("MM1", 2, 3, 2),
+    ("MM1", 2, 3, 3),
     ("MM2", 2, 3, 0),
     ("ACT", 2, 3, 0),
-    ("O", 2, (0, 1, 2, 3)),
-    ("ST", 2, (0, 1)),
-    ("ST", 2, (2, 3)),
-    ("MM1", 2, 3, 1),
     ("B", 3, (0,)),
     ("MM2", 2, 3, 1),
     ("ACT", 2, 3, 1),
     ("O", 3, (0,)),
     ("ST", 3, (0,)),
-    ("MM1", 2, 3, 2),
-    ("B", 3, (1,)),
     ("MM2", 2, 3, 2),
     ("ACT", 2, 3, 2),
-    ("O", 3, (1,)),
-    ("ST", 3, (1,)),
-    ("MM1", 2, 3, 3),
-    ("B", 3, (2,)),
+    ("B", 3, (1,)),
     ("MM2", 2, 3, 3),
     ("ACT", 2, 3, 3),
+    ("O", 3, (1,)),
+    ("ST", 3, (1,)),
+    ("B", 3, (2,)),
     ("O", 3, (2,)),
     ("ST", 3, (2,)),
     ("B", 3, (3,)),
@@ -410,7 +410,7 @@ def tile_gru_kernel(tc, x, h, w_r, b_r, w_u, b_u, w_h, b_h, out):
             b, lo, w = CHUNKS[c]
             if (g, c) not in gate:
                 nm = ("r_sb", "u_sb", "n_sb")[g]
-                gate[(g, c)] = rot.tile([P, T, w], F32, name=nm, tag=nm, bufs=(2, 2, 2)[g])
+                gate[(g, c)] = rot.tile([P, T, w], F32, name=nm, tag=nm, bufs=(2, 3, 2)[g])
             nc.scalar.activation(
                 out=gate[(g, c)][:, t, :], in_=bank[(g, c, t)][:, 0:w], func=funcs[g], bias=bias[g][:, t : t + 1], scale=1.0
             )

@@ -17,7 +17,7 @@ B = 2
 CH = 512
 L = 1024
 FLOPS = 2 * 3 * CH * (2 * CH) * B * L
-PIN = True
+PIN = False
 CHUNKS = ((0, 0, 512), (0, 512, 512), (1, 0, 512), (1, 512, 512))
 PLAN = [
     ("LD", "x", 0, 0),

@@ -16,265 +16,16 @@ T = 4
 B = 2
 CH = 512
 L = 1024
+CW = 512
+NCHUNK = B * L // CW
 FLOPS = 2 * 3 * CH * (2 * CH) * B * L
-PIN = False
-CHUNKS = ((0, 0, 512), (0, 512, 512), (1, 0, 512), (1, 512, 512))
-PLAN = [
-    ("LD", "x", 0, 0),
-    ("LD", "x", 0, 1),
-    ("LD", "h", 0, 0),
-    ("LD", "h", 0, 1),
-    ("LD", "w", 0, 0),
-    ("LD", "w", 0, 1),
-    ("LD", "x", 1, 0),
-    ("LD", "x", 1, 1),
-    ("LD", "h", 1, 0),
-    ("LD", "h", 1, 1),
-    ("LD", "w", 1, 0),
-    ("LD", "w", 1, 1),
-    ("LD", "w", 2, 0),
-    ("LD", "w", 2, 1),
-    ("LD", "x", 2, 0),
-    ("LD", "x", 2, 1),
-    ("LD", "h", 2, 0),
-    ("LD", "h", 2, 1),
-    ("LD", "x", 3, 0),
-    ("LD", "x", 3, 1),
-    ("LD", "h", 3, 0),
-    ("LD", "h", 3, 1),
-    ("WT", 0, 0),
-    ("G", "x", 0, "S"),
-    ("G", "h", 0, "V"),
-    ("WT", 0, 1),
-    ("WC", 0, 0, "S"),
-    ("Q", "x", 0),
-    ("WT", 0, 2),
-    ("WC", 0, 1, "S"),
-    ("Q", "h", 0),
-    ("WT", 0, 3),
-    ("WC", 0, 2, "S"),
-    ("WQ", 0, (0,)),
-    ("MM1", 0, 0, 0),
-    ("G", "x", 1, "S"),
-    ("WQ", 0, (1,)),
-    ("MM2", 0, 0, 0),
-    ("ACT", 0, 0, 0),
-    ("WC", 0, 3, "V"),
-    ("MM1", 0, 0, 1),
-    ("WQ", 0, (2,)),
-    ("MM2", 0, 0, 1),
-    ("ACT", 0, 0, 1),
-    ("WQ", 0, (3,)),
-    ("MM1", 0, 0, 2),
-    ("G", "h", 1, "V"),
-    ("MM2", 0, 0, 2),
-    ("ACT", 0, 0, 2),
-    ("Q", "h", 1),
-    ("MM1", 0, 0, 3),
-    ("Q", "x", 1),
-    ("MM2", 0, 0, 3),
-    ("ACT", 0, 0, 3),
-    ("WT", 1, 0),
-    ("WC", 1, 0, "V"),
-    ("WT", 1, 1),
-    ("WC", 1, 1, "S"),
-    ("WQ", 1, (0,)),
-    ("WT", 1, 2),
-    ("WC", 1, 2, "S"),
-    ("V1", 0),
-    ("WT", 1, 3),
-    ("WC", 1, 3, "S"),
-    ("WQ", 1, (1,)),
-    ("MM1", 0, 1, 0),
-    ("WQ", 1, (2,)),
-    ("WT", 2, 0),
-    ("WC", 2, 0, "S"),
-    ("WQ", 1, (3,)),
-    ("WT", 2, 1),
-    ("WC", 2, 1, "S"),
-    ("WQ", 2, (0,)),
-    ("MM2", 0, 1, 0),
-    ("WQ", 2, (1,)),
-    ("MM1", 1, 0, 0),
-    ("WT", 2, 2),
-    ("WC", 2, 2, "S"),
-    ("WQ", 2, (2,)),
-    ("WT", 2, 3),
-    ("WC", 2, 3, "S"),
-    ("WQ", 2, (3,)),
-    ("MM2", 1, 0, 0),
-    ("ACT", 1, 0, 0),
-    ("Q", "hr", 0),
-    ("MM1", 0, 1, 1),
-    ("ACT", 0, 1, 0),
-    ("G", "x", 2, "V"),
-    ("MM2", 0, 1, 1),
-    ("Q", "x", 2),
-    ("MM1", 0, 1, 2),
-    ("MM2", 0, 1, 2),
-    ("MM1", 1, 0, 1),
-    ("MM2", 1, 0, 1),
-    ("ACT", 1, 0, 1),
-    ("MM1", 1, 0, 2),
-    ("MM2", 1, 0, 2),
-    ("ACT", 1, 0, 2),
-    ("MM1", 1, 0, 3),
-    ("MM2", 1, 0, 3),
-    ("ACT", 1, 0, 3),
-    ("A", 0),
-    ("MM1", 0, 1, 3),
-    ("ACT", 0, 1, 1),
-    ("MM2", 0, 1, 3),
-    ("ACT", 0, 1, 2),
-    ("MM1", 2, 0, 0),
-    ("ACT", 0, 1, 3),
-    ("V1", 1),
-    ("MM2", 2, 0, 0),
-    ("ACT", 2, 0, 0),
-    ("Q", "hr", 1),
-    ("MM1", 2, 0, 1),
-    ("MM2", 2, 0, 1),
-    ("ACT", 2, 0, 1),
-    ("MM1", 2, 0, 2),
-    ("MM2", 2, 0, 2),
-    ("ACT", 2, 0, 2),
-    ("MM1", 2, 0, 3),
-    ("MM2", 2, 0, 3),
-    ("ACT", 2, 0, 3),
-    ("B", 0, (0, 1, 2, 3)),
-    ("MM1", 1, 1, 0),
-    ("G", "h", 2, "S"),
-    ("Q", "h", 2),
-    ("MM2", 1, 1, 0),
-    ("ACT", 1, 1, 0),
-    ("O", 0, (0, 1, 2, 3)),
-    ("ST", 0, (0, 1)),
-    ("ST", 0, (2, 3)),
-    ("MM1", 1, 1, 1),
-    ("MM2", 1, 1, 1),
-    ("ACT", 1, 1, 1),
-    ("MM1", 1, 1, 2),
-    ("MM2", 1, 1, 2),
-    ("ACT", 1, 1, 2),
-    ("MM1", 1, 1, 3),
-    ("MM2", 1, 1, 3),
-    ("ACT", 1, 1, 3),
-    ("A", 1),
-    ("MM1", 0, 2, 0),
-    ("MM1", 0, 2, 1),
-    ("MM1", 0, 2, 2),
-    ("MM1", 0, 2, 3),
-    ("MM1", 2, 1, 0),
-    ("MM2", 2, 1, 0),
-    ("ACT", 2, 1, 0),
-    ("MM1", 2, 1, 1),
-    ("MM2", 2, 1, 1),
-    ("ACT", 2, 1, 1),
-    ("MM1", 2, 1, 2),
-    ("MM2", 2, 1, 2),
-    ("ACT", 2, 1, 2),
-    ("MM1", 2, 1, 3),
-    ("MM2", 2, 1, 3),
-    ("MM2", 0, 2, 0),
-    ("ACT", 0, 2, 0),
-    ("MM2", 0, 2, 1),
-    ("ACT", 0, 2, 1),
-    ("MM2", 0, 2, 2),
-    ("ACT", 0, 2, 2),
-    ("MM2", 0, 2, 3),
-    ("ACT", 0, 2, 3),
-    ("V1", 2),
-    ("MM1", 1, 2, 0),
-    ("ACT", 2, 1, 3),
-    ("Q", "hr", 2),
-    ("MM2", 1, 2, 0),
-    ("G", "x", 3, "S"),
-    ("Q", "x", 3),
-    ("MM1", 1, 2, 1),
-    ("G", "h", 3, "S"),
-    ("B", 1, (0, 1, 2, 3)),
-    ("MM2", 1, 2, 1),
-    ("ACT", 1, 2, 0),
-    ("Q", "h", 3),
-    ("MM1", 1, 2, 2),
-    ("ACT", 1, 2, 1),
-    ("O", 1, (0, 1, 2, 3)),
-    ("ST", 1, (0, 1)),
-    ("ST", 1, (2, 3)),
-    ("MM2", 1, 2, 2),
-    ("ACT", 1, 2, 2),
-    ("MM1", 1, 2, 3),
-    ("MM2", 1, 2, 3),
-    ("ACT", 1, 2, 3),
-    ("A", 2),
-    ("MM1", 2, 2, 0),
-    ("MM1", 2, 2, 1),
-    ("MM1", 2, 2, 2),
-    ("MM1", 2, 2, 3),
-    ("MM2", 2, 2, 0),
-    ("ACT", 2, 2, 0),
-    ("MM2", 2, 2, 1),
-    ("ACT", 2, 2, 1),
-    ("MM2", 2, 2, 2),
-    ("MM2", 2, 2, 3),
-    ("MM1", 0, 3, 0),
-    ("MM1", 0, 3, 1),
-    ("MM1", 0, 3, 2),
-    ("MM1", 0, 3, 3),
-    ("MM2", 0, 3, 0),
-    ("ACT", 0, 3, 0),
-    ("MM2", 0, 3, 1),
-    ("ACT", 0, 3, 1),
-    ("MM2", 0, 3, 2),
-    ("ACT", 0, 3, 2),
-    ("MM2", 0, 3, 3),
-    ("ACT", 0, 3, 3),
-    ("V1", 3),
-    ("MM1", 1, 3, 0),
-    ("ACT", 2, 2, 2),
-    ("Q", "hr", 3),
-    ("MM2", 1, 3, 0),
-    ("ACT", 2, 2, 3),
-    ("B", 2, (0, 1, 2, 3)),
-    ("MM1", 1, 3, 1),
-    ("ACT", 1, 3, 0),
-    ("O", 2, (0, 1, 2, 3)),
-    ("ST", 2, (0, 1)),
-    ("ST", 2, (2, 3)),
-    ("MM2", 1, 3, 1),
-    ("ACT", 1, 3, 1),
-    ("MM1", 1, 3, 2),
-    ("MM2", 1, 3, 2),
-    ("ACT", 1, 3, 2),
-    ("MM1", 1, 3, 3),
-    ("MM2", 1, 3, 3),
-    ("ACT", 1, 3, 3),
-    ("A", 3),
-    ("MM1", 2, 3, 0),
-    ("MM1", 2, 3, 1),
-    ("MM1", 2, 3, 2),
-    ("MM1", 2, 3, 3),
-    ("MM2", 2, 3, 0),
-    ("ACT", 2, 3, 0),
-    ("B", 3, (0,)),
-    ("MM2", 2, 3, 1),
-    ("ACT", 2, 3, 1),
-    ("O", 3, (0,)),
-    ("ST", 3, (0,)),
-    ("MM2", 2, 3, 2),
-    ("ACT", 2, 3, 2),
-    ("B", 3, (1,)),
-    ("MM2", 2, 3, 3),
-    ("ACT", 2, 3, 3),
-    ("O", 3, (1,)),
-    ("ST", 3, (1,)),
-    ("B", 3, (2,)),
-    ("O", 3, (2,)),
-    ("ST", 3, (2,)),
-    ("B", 3, (3,)),
-    ("O", 3, (3,)),
-    ("ST", 3, (3,)),
-]
+
+R = 0
+U = 1
+N = 2
+
+VECTOR_REGROUPS = (("h", 0), ("h", 1), ("x", 2))
+VECTOR_WEIGHT_COPIES = ((R, 3), (U, 0))
 
 
 def tile_gru_kernel(tc, x, h, w_r, b_r, w_u, b_u, w_h, b_h, out):
@@ -313,6 +64,20 @@ def tile_gru_kernel(tc, x, h, w_r, b_r, w_u, b_u, w_h, b_h, out):
         def rows(ap2d):
             return ap2d.rearrange("(u p e) l -> p u e l", u=2, p=P, e=2)
 
+        def where(c):
+            return (c * CW) // L, (c * CW) % L
+
+        def load_act(nm, c):
+            b, lo = where(c)
+            for u in range(2):
+                nc.sync.dma_start(
+                    out=raw[(nm, b)][:, 2 * u : 2 * u + 2, lo : lo + CW], in_=rows(dram[nm][b])[:, u, :, lo : lo + CW]
+                )
+
+        def load_w(g):
+            for u in range(2):
+                nc.sync.dma_start(out=w_sb[g][:, 2 * u : 2 * u + 2, :], in_=rows(weights[g])[:, u, :, :])
+
         for g in range(3):
             nc.scalar.dma_start(
                 out=bias_bf[g][:].rearrange("p (u e) -> p u e", u=2),
@@ -321,172 +86,144 @@ def tile_gru_kernel(tc, x, h, w_r, b_r, w_u, b_u, w_h, b_h, out):
         for g in range(3):
             nc.vector.tensor_copy(out=bias[g][:], in_=bias_bf[g][:])
 
+        load_act("x", 0)
+        load_act("h", 0)
+        load_w(R)
+        load_act("x", 1)
+        load_act("h", 1)
+        load_w(U)
+        load_w(N)
+        for c in range(2, NCHUNK):
+            load_act("x", c)
+            load_act("h", c)
+
         grp = {}
-        w_grp = {}
-        bank = {}
         gate = {}
         mix = {}
 
-        def gcol(c):
-            b, lo, w = CHUNKS[c]
-            return b * L + lo
-
-        def do_ld(kind, a, u):
-            if kind == "w":
-                nc.sync.dma_start(out=w_sb[a][:, 2 * u : 2 * u + 2, :], in_=rows(weights[a])[:, u, :, :])
-            else:
-                b, lo, w = CHUNKS[a]
-                nc.sync.dma_start(
-                    out=raw[(kind, b)][:, 2 * u : 2 * u + 2, lo : lo + w], in_=rows(dram[kind][b])[:, u, :, lo : lo + w]
-                )
-
-        def do_g(nm, c, e):
-            b, lo, w = CHUNKS[c]
+        def regroup(nm, c):
+            b, lo = where(c)
             if nm == "x":
-                dst = rot.tile([P, w, T], BF16, name="x_grp", tag="x_grp", bufs=2, align_bytes=64)
+                dst = rot.tile([P, CW, T], BF16, name="x_grp", tag="x_grp", bufs=2, align_bytes=64)
             else:
-                dst = keep.tile([P, w, T], BF16, name="h_grp%d" % c, align_bytes=64)
+                dst = keep.tile([P, CW, T], BF16, name="h_grp%d" % c, align_bytes=64)
             grp[(nm, c)] = dst
             o_ap = dst[:].rearrange("p (c i) t -> p c t i", i=4)
-            i_ap = raw[(nm, b)][:, :, lo : lo + w].rearrange("p t (c i) -> p c t i", i=4)
-            if e == "V":
+            i_ap = raw[(nm, b)][:, :, lo : lo + CW].rearrange("p t (c i) -> p c t i", i=4)
+            if (nm, c) in VECTOR_REGROUPS:
                 nc.vector.tensor_copy(out=o_ap, in_=i_ap)
             else:
                 nc.scalar.copy(out=o_ap, in_=i_ap)
 
-        def do_q(nm, c):
-            b, lo, w = CHUNKS[c]
-            g0 = gcol(c)
+        def quantise(nm, c):
             nc.vector.quantize_mx(
-                out=codes[nm][:, g0 : g0 + w].bitcast(FP8X4),
-                scales=scales[nm][:, g0 : g0 + w],
+                out=codes[nm][:, c * CW : (c + 1) * CW].bitcast(FP8X4),
+                scales=scales[nm][:, c * CW : (c + 1) * CW],
                 in_=grp[(nm, c)][:].rearrange("p l t -> p (l t)"),
             )
 
-        def do_wt(g, t):
+        def prepare_weight(g):
             w32 = w_sb[g][:].bitcast(F32)
-            bk = psum.tile([P, 4, P], F32, name="bank", tag="bank")
-            bank[("w", g, t)] = bk
-            for a in range(4):
-                nc.tensor.transpose(bk[:, a, :], w32[:, t, a * P : (a + 1) * P], ident[:])
+            w_grp = rot.tile([P, T * 2 * P * 4], BF16, name="w_grp", tag="w_grp", bufs=2, align_bytes=64)
+            g32 = w_grp[:].bitcast(F32).rearrange("p (t g o u) -> p t g o u", t=T, g=2, o=P, u=2)
+            banks = []
+            for t in range(T):
+                bk = psum.tile([P, 4, P], F32, name="bank", tag="bank")
+                banks.append(bk)
+                for a in range(4):
+                    nc.tensor.transpose(bk[:, a, :], w32[:, t, a * P : (a + 1) * P], ident[:])
+            for t in range(T):
+                src = banks[t][:].rearrange("p (g u) o -> p g o u", g=2)
+                if (g, t) in VECTOR_WEIGHT_COPIES:
+                    nc.vector.tensor_copy(out=g32[:, t], in_=src)
+                else:
+                    nc.scalar.copy(out=g32[:, t], in_=src)
+                nc.vector.quantize_mx(
+                    out=wq[g][:, t * 2 * P : (t + 1) * 2 * P].bitcast(FP8X4),
+                    scales=ws[g][:, t * 2 * P : (t + 1) * 2 * P],
+                    in_=w_grp[:, t * 8 * P : (t + 1) * 8 * P],
+                )
 
-        def do_wc(g, t, e):
-            if g not in w_grp:
-                w_grp[g] = rot.tile([P, T * 2 * P * 4], BF16, name="w_grp", tag="w_grp", bufs=2, align_bytes=64)
-            g32 = w_grp[g][:].bitcast(F32).rearrange("p (t g o u) -> p t g o u", t=T, g=2, o=P, u=2)
-            src = bank[("w", g, t)][:].rearrange("p (g u) o -> p g o u", g=2)
-            if e == "V":
-                nc.vector.tensor_copy(out=g32[:, t], in_=src)
-            else:
-                nc.scalar.copy(out=g32[:, t], in_=src)
+        def conv(g, c):
+            nm_tile = ("r_sb", "u_sb", "n_sb")[g]
+            dst = rot.tile([P, T, CW], F32, name=nm_tile, tag=nm_tile, bufs=(2, 3, 2)[g])
+            gate[(g, c)] = dst
+            banks = []
+            for k in range(2):
+                nm = "x" if k == 0 else ("hr" if g == N else "h")
+                for t in range(T):
+                    if k == 0:
+                        banks.append(psum.tile([P, CW], F32, name="bank", tag="bank"))
+                    wsl = slice((t * 2 + k) * P, (t * 2 + k + 1) * P)
+                    nc.tensor.matmul_mx(
+                        out=banks[t][:],
+                        lhsT=wq[g][:, wsl].bitcast(FP8X4),
+                        lhsT_scale=ws[g][:, wsl],
+                        rhs=codes[nm][:, c * CW : (c + 1) * CW].bitcast(FP8X4),
+                        rhs_scale=scales[nm][:, c * CW : (c + 1) * CW],
+                        start=(k == 0),
+                        stop=(k == 1),
+                    )
+            for t in range(T):
+                nc.scalar.activation(out=dst[:, t, :], in_=banks[t][:], func=funcs[g], bias=bias[g][:, t : t + 1], scale=1.0)
 
-        def do_wq(g, ts):
-            t0 = ts[0]
-            n = len(ts)
-            nc.vector.quantize_mx(
-                out=wq[g][:, t0 * 2 * P : (t0 + n) * 2 * P].bitcast(FP8X4),
-                scales=ws[g][:, t0 * 2 * P : (t0 + n) * 2 * P],
-                in_=w_grp[g][:, t0 * 8 * P : (t0 + n) * 8 * P],
-            )
-
-        def do_mm(g, c, t, k):
-            b, lo, w = CHUNKS[c]
-            g0 = gcol(c)
-            if k == 0:
-                bank[(g, c, t)] = psum.tile([P, 512], F32, name="bank", tag="bank")
-            nm = "x" if k == 0 else ("hr" if g == 2 else "h")
-            wsl = slice((t * 2 + k) * P, (t * 2 + k + 1) * P)
-            nc.tensor.matmul_mx(
-                out=bank[(g, c, t)][:, 0:w],
-                lhsT=wq[g][:, wsl].bitcast(FP8X4),
-                lhsT_scale=ws[g][:, wsl],
-                rhs=codes[nm][:, g0 : g0 + w].bitcast(FP8X4),
-                rhs_scale=scales[nm][:, g0 : g0 + w],
-                start=(k == 0),
-                stop=(k == 1),
-            )
-
-        def do_act(g, c, t):
-            b, lo, w = CHUNKS[c]
-            if (g, c) not in gate:
-                nm = ("r_sb", "u_sb", "n_sb")[g]
-                gate[(g, c)] = rot.tile([P, T, w], F32, name=nm, tag=nm, bufs=(2, 3, 2)[g])
-            nc.scalar.activation(
-                out=gate[(g, c)][:, t, :], in_=bank[(g, c, t)][:, 0:w], func=funcs[g], bias=bias[g][:, t : t + 1], scale=1.0
-            )
-
-        def do_v1(c):
-            b, lo, w = CHUNKS[c]
-            dst = rot.tile([P, w, T], BF16, name="hr_grp", tag="hr_grp", bufs=2, align_bytes=64)
+        def reset(c):
+            dst = rot.tile([P, CW, T], BF16, name="hr_grp", tag="hr_grp", bufs=2, align_bytes=64)
             grp[("hr", c)] = dst
             nc.vector.tensor_tensor(
-                out=dst[:], in0=grp[("h", c)][:], in1=gate[(0, c)][:].rearrange("p t l -> p l t"), op=ALU.mult
+                out=dst[:], in0=grp[("h", c)][:], in1=gate[(R, c)][:].rearrange("p t l -> p l t"), op=ALU.mult
             )
 
-        def do_a(c):
-            b, lo, w = CHUNKS[c]
-            mix[c] = rot.tile([P, T, w], F32, name="a_sb", tag="a_sb", bufs=3)
-            nc.vector.tensor_tensor(out=mix[c][:], in0=gate[(1, c)][:], in1=raw[("h", b)][:, :, lo : lo + w], op=ALU.mult)
+        def mix_a(c):
+            b, lo = where(c)
+            mix[c] = rot.tile([P, T, CW], F32, name="a_sb", tag="a_sb", bufs=3)
+            nc.vector.tensor_tensor(out=mix[c][:], in0=gate[(U, c)][:], in1=raw[("h", b)][:, :, lo : lo + CW], op=ALU.mult)
 
-        def flat(ap, ts):
-            return ap[:, ts[0] : ts[0] + len(ts), :].rearrange("p t l -> p (t l)")
-
-        def do_b(c, ts):
-            nf = flat(gate[(2, c)], ts)
-            nc.vector.scalar_tensor_tensor(
-                out=nf, in0=flat(gate[(1, c)], ts), scalar=1.0, in1=nf, op0=ALU.subtract, op1=ALU.mult
-            )
-
-        def do_o(c, ts):
-            af = flat(mix[c], ts)
-            nc.vector.tensor_tensor(out=af, in0=af, in1=flat(gate[(2, c)], ts), op=ALU.subtract)
-
-        def do_st(c, ts):
-            b, lo, w = CHUNKS[c]
+        def mix_out(c, step):
+            b, lo = where(c)
             view = rows(out[b])
-            if len(ts) == 2:
-                u = ts[0] // 2
-                nc.sync.dma_start(out=view[:, u, :, lo : lo + w], in_=mix[c][:, 2 * u : 2 * u + 2, :])
-            else:
-                t = ts[0]
-                nc.sync.dma_start(out=view[:, t // 2, t % 2, lo : lo + w], in_=mix[c][:, t, :])
-
-        def run_plan():
-            for op in PLAN:
-                k = op[0]
-                if k == "LD":
-                    do_ld(op[1], op[2], op[3])
-                elif k == "G":
-                    do_g(op[1], op[2], op[3])
-                elif k == "Q":
-                    do_q(op[1], op[2])
-                elif k == "WT":
-                    do_wt(op[1], op[2])
-                elif k == "WC":
-                    do_wc(op[1], op[2], op[3])
-                elif k == "WQ":
-                    do_wq(op[1], op[2])
-                elif k == "MM1":
-                    do_mm(op[1], op[2], op[3], 0)
-                elif k == "MM2":
-                    do_mm(op[1], op[2], op[3], 1)
-                elif k == "ACT":
-                    do_act(op[1], op[2], op[3])
-                elif k == "V1":
-                    do_v1(op[1])
-                elif k == "A":
-                    do_a(op[1])
-                elif k == "B":
-                    do_b(op[1], op[2])
-                elif k == "O":
-                    do_o(op[1], op[2])
-                elif k == "ST":
-                    do_st(op[1], op[2])
+            for t0 in range(0, T, step):
+                nf = gate[(N, c)][:, t0 : t0 + step, :].rearrange("p t l -> p (t l)")
+                uf = gate[(U, c)][:, t0 : t0 + step, :].rearrange("p t l -> p (t l)")
+                af = mix[c][:, t0 : t0 + step, :].rearrange("p t l -> p (t l)")
+                nc.vector.scalar_tensor_tensor(out=nf, in0=uf, scalar=1.0, in1=nf, op0=ALU.subtract, op1=ALU.mult)
+                nc.vector.tensor_tensor(out=af, in0=af, in1=nf, op=ALU.subtract)
+                if step == 1:
+                    nc.sync.dma_start(out=view[:, t0 // 2, t0 % 2, lo : lo + CW], in_=mix[c][:, t0, :])
                 else:
-                    raise ValueError(k)
+                    for u in range(t0 // 2, (t0 + step) // 2):
+                        nc.sync.dma_start(out=view[:, u, :, lo : lo + CW], in_=mix[c][:, 2 * u : 2 * u + 2, :])
 
-        if PIN:
-            with tc.manual_schedule():
-                run_plan()
-        else:
-            run_plan()
+        regroup("x", 0)
+        regroup("h", 0)
+        quantise("x", 0)
+        quantise("h", 0)
+        prepare_weight(R)
+        regroup("x", 1)
+        regroup("h", 1)
+        quantise("h", 1)
+        quantise("x", 1)
+        conv(R, 0)
+        prepare_weight(U)
+        reset(0)
+        prepare_weight(N)
+        quantise("hr", 0)
+        conv(U, 0)
+        for c in range(1, NCHUNK):
+            conv(R, c)
+            if c + 1 < NCHUNK:
+                regroup("x", c + 1)
+                quantise("x", c + 1)
+            mix_a(c - 1)
+            conv(N, c - 1)
+            reset(c)
+            quantise("hr", c)
+            if c + 1 < NCHUNK:
+                regroup("h", c + 1)
+            conv(U, c)
+            if c + 1 < NCHUNK:
+                quantise("h", c + 1)
+            mix_out(c - 1, T)
+        conv(N, NCHUNK - 1)
+        mix_a(NCHUNK - 1)
+        mix_out(NCHUNK - 1, 1)

@@ -16,8 +16,9 @@ T = 4
 B = 2
 CH = 512
 L = 1024
-CW = 512
-NCHUNK = B * L // CW
+CHUNKS = ((0, 0, 512), (0, 512, 512), (1, 0, 512), (1, 512, 512))
+LOADS = (("a", 0, 0, 1024), ("w", 0), ("w", 1), ("w", 2), ("a", 1, 0, 1024))
+NCHUNK = len(CHUNKS)
 FLOPS = 2 * 3 * CH * (2 * CH) * B * L
 
 R = 0
@@ -64,14 +65,10 @@ def tile_gru_kernel(tc, x, h, w_r, b_r, w_u, b_u, w_h, b_h, out):
         def rows(ap2d):
             return ap2d.rearrange("(u p e) l -> p u e l", u=2, p=P, e=2)
 
-        def where(c):
-            return (c * CW) // L, (c * CW) % L
-
-        def load_act(nm, c):
-            b, lo = where(c)
+        def load_act(nm, b, lo, w):
             for u in range(2):
                 nc.sync.dma_start(
-                    out=raw[(nm, b)][:, 2 * u : 2 * u + 2, lo : lo + CW], in_=rows(dram[nm][b])[:, u, :, lo : lo + CW]
+                    out=raw[(nm, b)][:, 2 * u : 2 * u + 2, lo : lo + w], in_=rows(dram[nm][b])[:, u, :, lo : lo + w]
                 )
 
         def load_w(g):
@@ -86,23 +83,19 @@ def tile_gru_kernel(tc, x, h, w_r, b_r, w_u, b_u, w_h, b_h, out):
         for g in range(3):
             nc.vector.tensor_copy(out=bias[g][:], in_=bias_bf[g][:])
 
-        load_act("x", 0)
-        load_act("h", 0)
-        load_w(R)
-        load_act("x", 1)
-        load_act("h", 1)
-        load_w(U)
-        load_w(N)
-        for c in range(2, NCHUNK):
-            load_act("x", c)
-            load_act("h", c)
+        for item in LOADS:
+            if item[0] == "w":
+                load_w(item[1])
+            else:
+                load_act("x", item[1], item[2], item[3])
+                load_act("h", item[1], item[2], item[3])
 
         grp = {}
         gate = {}
         mix = {}
 
         def regroup(nm, c):
-            b, lo = where(c)
+            b, lo, CW = CHUNKS[c]
             if nm == "x":
                 dst = rot.tile([P, CW, T], BF16, name="x_grp", tag="x_grp", bufs=2, align_bytes=64)
             else:
@@ -116,9 +109,11 @@ def tile_gru_kernel(tc, x, h, w_r, b_r, w_u, b_u, w_h, b_h, out):
                 nc.scalar.copy(out=o_ap, in_=i_ap)
 
         def quantise(nm, c):
+            b, lo, CW = CHUNKS[c]
+            g0 = b * L + lo
             nc.vector.quantize_mx(
-                out=codes[nm][:, c * CW : (c + 1) * CW].bitcast(FP8X4),
-                scales=scales[nm][:, c * CW : (c + 1) * CW],
+                out=codes[nm][:, g0 : g0 + CW].bitcast(FP8X4),
+                scales=scales[nm][:, g0 : g0 + CW],
                 in_=grp[(nm, c)][:].rearrange("p l t -> p (l t)"),
             )
 
@@ -145,6 +140,8 @@ def tile_gru_kernel(tc, x, h, w_r, b_r, w_u, b_u, w_h, b_h, out):
                 )
 
         def conv(g, c):
+            b, lo, CW = CHUNKS[c]
+            g0 = b * L + lo
             nm_tile = ("r_sb", "u_sb", "n_sb")[g]
             dst = rot.tile([P, T, CW], F32, name=nm_tile, tag=nm_tile, bufs=(2, 3, 2)[g])
             gate[(g, c)] = dst
@@ -153,21 +150,22 @@ def tile_gru_kernel(tc, x, h, w_r, b_r, w_u, b_u, w_h, b_h, out):
                 nm = "x" if k == 0 else ("hr" if g == N else "h")
                 for t in range(T):
                     if k == 0:
-                        banks.append(psum.tile([P, CW], F32, name="bank", tag="bank"))
+                        banks.append(psum.tile([P, 512], F32, name="bank", tag="bank"))
                     wsl = slice((t * 2 + k) * P, (t * 2 + k + 1) * P)
                     nc.tensor.matmul_mx(
-                        out=banks[t][:],
+                        out=banks[t][:, 0:CW],
                         lhsT=wq[g][:, wsl].bitcast(FP8X4),
                         lhsT_scale=ws[g][:, wsl],
-                        rhs=codes[nm][:, c * CW : (c + 1) * CW].bitcast(FP8X4),
-                        rhs_scale=scales[nm][:, c * CW : (c + 1) * CW],
+                        rhs=codes[nm][:, g0 : g0 + CW].bitcast(FP8X4),
+                        rhs_scale=scales[nm][:, g0 : g0 + CW],
                         start=(k == 0),
                         stop=(k == 1),
                     )
             for t in range(T):
-                nc.scalar.activation(out=dst[:, t, :], in_=banks[t][:], func=funcs[g], bias=bias[g][:, t : t + 1], scale=1.0)
+                nc.scalar.activation(out=dst[:, t, :], in_=banks[t][:, 0:CW], func=funcs[g], bias=bias[g][:, t : t + 1], scale=1.0)
 
         def reset(c):
+            b, lo, CW = CHUNKS[c]
             dst = rot.tile([P, CW, T], BF16, name="hr_grp", tag="hr_grp", bufs=2, align_bytes=64)
             grp[("hr", c)] = dst
             nc.vector.tensor_tensor(
@@ -175,12 +173,12 @@ def tile_gru_kernel(tc, x, h, w_r, b_r, w_u, b_u, w_h, b_h, out):
             )
 
         def mix_a(c):
-            b, lo = where(c)
+            b, lo, CW = CHUNKS[c]
             mix[c] = rot.tile([P, T, CW], F32, name="a_sb", tag="a_sb", bufs=3)
             nc.vector.tensor_tensor(out=mix[c][:], in0=gate[(U, c)][:], in1=raw[("h", b)][:, :, lo : lo + CW], op=ALU.mult)
 
         def mix_out(c, step):
-            b, lo = where(c)
+            b, lo, CW = CHUNKS[c]
             view = rows(out[b])
             for t0 in range(0, T, step):
                 nf = gate[(N, c)][:, t0 : t0 + step, :].rearrange("p t l -> p (t l)")

@@ -25,7 +25,7 @@ R = 0
 U = 1
 N = 2
 
-VECTOR_REGROUPS = (("h", 0), ("h", 1), ("x", 2))
+VECTOR_REGROUPS = (("x", 1), ("h", 0), ("h", 1), ("x", 2))
 VECTOR_WEIGHT_COPIES = ((R, 3), (U, 0))
 
 

@@ -60,7 +60,6 @@ def tile_gru_kernel(tc, x, h, w_r, b_r, w_u, b_u, w_h, b_h, out):
             codes[nm] = keep.tile([P, B * L], U32, name="codes_%s" % nm, align_bytes=64)
             scales[nm] = keep.tile([P, B * L], U8, name="scales_%s" % nm, align_bytes=64)
         bias_bf = [keep.tile([P, T], BF16, name="bias_bf%d" % g) for g in range(3)]
-        bias = [keep.tile([P, T], F32, name="bias%d" % g) for g in range(3)]
 
         def rows(ap2d):
             return ap2d.rearrange("(u p e) l -> p u e l", u=2, p=P, e=2)
@@ -80,8 +79,6 @@ def tile_gru_kernel(tc, x, h, w_r, b_r, w_u, b_u, w_h, b_h, out):
                 out=bias_bf[g][:].rearrange("p (u e) -> p u e", u=2),
                 in_=biases[g].rearrange("(u p e) -> p u e", u=2, p=P, e=2),
             )
-        for g in range(3):
-            nc.vector.tensor_copy(out=bias[g][:], in_=bias_bf[g][:])
 
         for item in LOADS:
             if item[0] == "w":
@@ -162,14 +159,17 @@ def tile_gru_kernel(tc, x, h, w_r, b_r, w_u, b_u, w_h, b_h, out):
                         stop=(k == 1),
                     )
             for t in range(T):
-                nc.scalar.activation(out=dst[:, t, :], in_=banks[t][:, 0:CW], func=funcs[g], bias=bias[g][:, t : t + 1], scale=1.0)
+                nc.scalar.activation(out=dst[:, t, :], in_=banks[t][:, 0:CW], func=funcs[g], bias=bias_bf[g][:, t : t + 1], scale=1.0)
 
         def reset(c):
             b, lo, CW = CHUNKS[c]
             dst = rot.tile([P, CW, T], BF16, name="hr_grp", tag="hr_grp", bufs=2, align_bytes=64)
             grp[("hr", c)] = dst
             nc.vector.tensor_tensor(
-                out=dst[:], in0=grp[("h", c)][:], in1=gate[(R, c)][:].rearrange("p t l -> p l t"), op=ALU.mult
+                out=dst[:].rearrange("p (c i) t -> p c t i", i=4),
+                in0=grp[("h", c)][:].rearrange("p (c i) t -> p c t i", i=4),
+                in1=gate[(R, c)][:].rearrange("p t (c i) -> p c t i", i=4),
+                op=ALU.mult,
             )
 
         def mix_a(c):

@@ -16,16 +16,17 @@ T = 4
 B = 2
 CH = 512
 L = 1024
-CHUNKS = ((0, 0, 512), (0, 512, 512), (1, 0, 512), (1, 512, 512))
+CHUNKS = tuple((b, lo, 256) for b in range(2) for lo in range(0, 1024, 256))
 LOADS = (("a", 0, 0, 1024), ("w", 0), ("w", 1), ("w", 2), ("a", 1, 0, 1024))
 NCHUNK = len(CHUNKS)
+DIFF = (1, 3, 5, 7)
 FLOPS = 2 * 3 * CH * (2 * CH) * B * L
 
 R = 0
 U = 1
 N = 2
 
-VECTOR_REGROUPS = (("x", 1), ("h", 0), ("h", 1), ("x", 2))
+VECTOR_REGROUPS = (("x", 1), ("h", 0), ("h", 1), ("x", 2), ("x", 3), ("h", 3), ("x", 5), ("h", 5))
 VECTOR_WEIGHT_COPIES = ((R, 3), (U, 0))
 
 
@@ -45,6 +46,8 @@ def tile_gru_kernel(tc, x, h, w_r, b_r, w_u, b_u, w_h, b_h, out):
         nc.scalar.activation(out=warm_out[:], in_=warm[:], func=ACT.Sigmoid)
         ident = keep.tile([P, P], F32, name="ident")
         make_identity(nc, ident[:])
+        minus = keep.tile([P, P], BF16, name="minus")
+        nc.gpsimd.tensor_scalar(out=minus[:], in0=ident[:], scalar1=-1.0, scalar2=0.0, op0=ALU.mult, op1=ALU.add)
 
         raw = {}
         for nm in ("x", "h"):
@@ -114,18 +117,22 @@ def tile_gru_kernel(tc, x, h, w_r, b_r, w_u, b_u, w_h, b_h, out):
                 in_=grp[(nm, c)][:].rearrange("p l t -> p (l t)"),
             )
 
-        def prepare_weight(g):
+        turned = {}
+
+        def turn_weight(g):
             w32 = w_sb[g][:].bitcast(F32)
-            w_grp = rot.tile([P, T * 2 * P * 4], BF16, name="w_grp", tag="w_grp", bufs=2, align_bytes=64)
-            g32 = w_grp[:].bitcast(F32).rearrange("p (t g o u) -> p t g o u", t=T, g=2, o=P, u=2)
-            banks = []
+            turned[g] = []
             for t in range(T):
                 bk = psum.tile([P, 4, P], F32, name="bank", tag="bank")
-                banks.append(bk)
+                turned[g].append(bk)
                 for a in range(4):
                     nc.tensor.transpose(bk[:, a, :], w32[:, t, a * P : (a + 1) * P], ident[:])
+
+        def finish_weight(g):
+            w_grp = rot.tile([P, T * 2 * P * 4], BF16, name="w_grp", tag="w_grp", bufs=2, align_bytes=64)
+            g32 = w_grp[:].bitcast(F32).rearrange("p (t g o u) -> p t g o u", t=T, g=2, o=P, u=2)
             for t in range(T):
-                src = banks[t][:].rearrange("p (g u) o -> p g o u", g=2)
+                src = turned[g][t][:].rearrange("p (g u) o -> p g o u", g=2)
                 if (g, t) in VECTOR_WEIGHT_COPIES:
                     nc.vector.tensor_copy(out=g32[:, t], in_=src)
                 else:
@@ -192,19 +199,53 @@ def tile_gru_kernel(tc, x, h, w_r, b_r, w_u, b_u, w_h, b_h, out):
                     for u in range(t0 // 2, (t0 + step) // 2):
                         nc.sync.dma_start(out=view[:, u, :, lo : lo + CW], in_=mix[c][:, 2 * u : 2 * u + 2, :])
 
+        diff = {}
+
+        def make_diff(c):
+            b, lo, CW = CHUNKS[c]
+            for u in range(2):
+                bank = psum.tile([P, 2, CW], F32, name="bank", tag="bank")
+                diff[(c, u)] = bank
+                for e in range(2):
+                    t = 2 * u + e
+                    nc.tensor.matmul(
+                        bank[:, e, :], lhsT=minus[:], rhs=raw[("h", b)][:, t, lo : lo + CW], start=True, stop=False
+                    )
+                    nc.tensor.matmul(bank[:, e, :], lhsT=ident[:], rhs=gate[(N, c)][:, t, :], start=False, stop=True)
+
+        def scale_diff(c, u):
+            ut = gate[(U, c)][:, 2 * u : 2 * u + 2, :]
+            nc.vector.tensor_tensor(out=ut, in0=ut, in1=diff[(c, u)][:], op=ALU.mult)
+
+        def sub_store(c, u):
+            b, lo, CW = CHUNKS[c]
+            ut = gate[(U, c)][:, 2 * u : 2 * u + 2, :]
+            nt = gate[(N, c)][:, 2 * u : 2 * u + 2, :]
+            nc.vector.tensor_tensor(out=nt, in0=nt, in1=ut, op=ALU.subtract)
+            nc.sync.dma_start(out=rows(out[b])[:, u, :, lo : lo + CW], in_=nt)
+
+        def finish_diff(c):
+            scale_diff(c, 0)
+            scale_diff(c, 1)
+            sub_store(c, 0)
+            sub_store(c, 1)
+
         regroup("x", 0)
         regroup("h", 0)
         quantise("x", 0)
         quantise("h", 0)
-        prepare_weight(R)
+        turn_weight(R)
+        finish_weight(R)
         regroup("x", 1)
         regroup("h", 1)
         quantise("h", 1)
         quantise("x", 1)
+        turn_weight(U)
         conv(R, 0)
-        prepare_weight(U)
+        finish_weight(U)
         reset(0)
-        prepare_weight(N)
+        turn_weight(N)
+        finish_weight(N)
         quantise("hr", 0)
         conv(U, 0)
         for c in range(1, NCHUNK):
@@ -212,16 +253,22 @@ def tile_gru_kernel(tc, x, h, w_r, b_r, w_u, b_u, w_h, b_h, out):
             if c + 1 < NCHUNK:
                 regroup("x", c + 1)
                 quantise("x", c + 1)
-            mix_a(c - 1)
+            if c - 1 not in DIFF:
+                mix_a(c - 1)
             conv(N, c - 1)
             reset(c)
             quantise("hr", c)
             if c + 1 < NCHUNK:
                 regroup("h", c + 1)
             conv(U, c)
+            if c - 1 in DIFF:
+                make_diff(c - 1)
             if c + 1 < NCHUNK:
                 quantise("h", c + 1)
-            mix_out(c - 1, T)
+            if c - 1 in DIFF:
+                finish_diff(c - 1)
+            else:
+                mix_out(c - 1, T)
         conv(N, NCHUNK - 1)
-        mix_a(NCHUNK - 1)
-        mix_out(NCHUNK - 1, 1)
+        make_diff(NCHUNK - 1)
+        finish_diff(NCHUNK - 1)

@@ -16,17 +16,17 @@ T = 4
 B = 2
 CH = 512
 L = 1024
-CHUNKS = tuple((b, lo, 256) for b in range(2) for lo in range(0, 1024, 256))
+CHUNKS = ((0, 0, 512), (0, 512, 512), (1, 0, 512), (1, 512, 256), (1, 768, 256))
 LOADS = (("a", 0, 0, 1024), ("w", 0), ("w", 1), ("w", 2), ("a", 1, 0, 1024))
 NCHUNK = len(CHUNKS)
-DIFF = (1, 3, 5, 7)
 FLOPS = 2 * 3 * CH * (2 * CH) * B * L
 
 R = 0
 U = 1
 N = 2
 
-VECTOR_REGROUPS = (("x", 1), ("h", 0), ("h", 1), ("x", 2), ("x", 3), ("h", 3), ("x", 5), ("h", 5))
+VECTOR_REGROUPS = (("x", 1), ("h", 0), ("h", 1), ("x", 2))
+W_STEP = (1, 2, 2)
 VECTOR_WEIGHT_COPIES = ((R, 3), (U, 0))
 
 
@@ -137,11 +137,13 @@ def tile_gru_kernel(tc, x, h, w_r, b_r, w_u, b_u, w_h, b_h, out):
                     nc.vector.tensor_copy(out=g32[:, t], in_=src)
                 else:
                     nc.scalar.copy(out=g32[:, t], in_=src)
-                nc.vector.quantize_mx(
-                    out=wq[g][:, t * 2 * P : (t + 1) * 2 * P].bitcast(FP8X4),
-                    scales=ws[g][:, t * 2 * P : (t + 1) * 2 * P],
-                    in_=w_grp[:, t * 8 * P : (t + 1) * 8 * P],
-                )
+                if t % W_STEP[g] == W_STEP[g] - 1:
+                    lo, hi = t + 1 - W_STEP[g], t + 1
+                    nc.vector.quantize_mx(
+                        out=wq[g][:, lo * 2 * P : hi * 2 * P].bitcast(FP8X4),
+                        scales=ws[g][:, lo * 2 * P : hi * 2 * P],
+                        in_=w_grp[:, lo * 8 * P : hi * 8 * P],
+                    )
 
         def conv(g, c):
             b, lo, CW = CHUNKS[c]
@@ -179,56 +181,53 @@ def tile_gru_kernel(tc, x, h, w_r, b_r, w_u, b_u, w_h, b_h, out):
                 op=ALU.mult,
             )
 
-        def mix_a(c):
-            b, lo, CW = CHUNKS[c]
-            mix[c] = rot.tile([P, T, CW], F32, name="a_sb", tag="a_sb", bufs=3)
-            nc.vector.tensor_tensor(out=mix[c][:], in0=gate[(U, c)][:], in1=raw[("h", b)][:, :, lo : lo + CW], op=ALU.mult)
-
-        def mix_out(c, step):
-            b, lo, CW = CHUNKS[c]
-            view = rows(out[b])
-            for t0 in range(0, T, step):
-                nf = gate[(N, c)][:, t0 : t0 + step, :].rearrange("p t l -> p (t l)")
-                uf = gate[(U, c)][:, t0 : t0 + step, :].rearrange("p t l -> p (t l)")
-                af = mix[c][:, t0 : t0 + step, :].rearrange("p t l -> p (t l)")
-                nc.vector.scalar_tensor_tensor(out=nf, in0=uf, scalar=1.0, in1=nf, op0=ALU.subtract, op1=ALU.mult)
-                nc.vector.tensor_tensor(out=af, in0=af, in1=nf, op=ALU.subtract)
-                if step == 1:
-                    nc.sync.dma_start(out=view[:, t0 // 2, t0 % 2, lo : lo + CW], in_=mix[c][:, t0, :])
-                else:
-                    for u in range(t0 // 2, (t0 + step) // 2):
-                        nc.sync.dma_start(out=view[:, u, :, lo : lo + CW], in_=mix[c][:, 2 * u : 2 * u + 2, :])
-
+        kept = {}
         diff = {}
+
+        def pair(tile, u):
+            return tile[:, 2 * u : 2 * u + 2, :]
+
+        def store(c, u, tile):
+            b, lo, CW = CHUNKS[c]
+            nc.sync.dma_start(out=rows(out[b])[:, u, :, lo : lo + CW], in_=tile)
 
         def make_diff(c):
             b, lo, CW = CHUNKS[c]
-            for u in range(2):
-                bank = psum.tile([P, 2, CW], F32, name="bank", tag="bank")
-                diff[(c, u)] = bank
-                for e in range(2):
-                    t = 2 * u + e
-                    nc.tensor.matmul(
-                        bank[:, e, :], lhsT=minus[:], rhs=raw[("h", b)][:, t, lo : lo + CW], start=True, stop=False
-                    )
-                    nc.tensor.matmul(bank[:, e, :], lhsT=ident[:], rhs=gate[(N, c)][:, t, :], start=False, stop=True)
+            for t in range(2):
+                if t == 0 or CW == 512:
+                    bank = psum.tile([P, 512 // CW, CW], F32, name="bank", tag="bank")
+                diff[(c, t)] = bank[:, t % (512 // CW), :]
+                nc.tensor.matmul(
+                    diff[(c, t)], lhsT=minus[:], rhs=raw[("h", b)][:, t, lo : lo + CW], start=True, stop=False
+                )
+                nc.tensor.matmul(diff[(c, t)], lhsT=ident[:], rhs=gate[(N, c)][:, t, :], start=False, stop=True)
 
-        def scale_diff(c, u):
-            ut = gate[(U, c)][:, 2 * u : 2 * u + 2, :]
-            nc.vector.tensor_tensor(out=ut, in0=ut, in1=diff[(c, u)][:], op=ALU.mult)
-
-        def sub_store(c, u):
+        def keep_old(c):
             b, lo, CW = CHUNKS[c]
-            ut = gate[(U, c)][:, 2 * u : 2 * u + 2, :]
-            nt = gate[(N, c)][:, 2 * u : 2 * u + 2, :]
-            nc.vector.tensor_tensor(out=nt, in0=nt, in1=ut, op=ALU.subtract)
-            nc.sync.dma_start(out=rows(out[b])[:, u, :, lo : lo + CW], in_=nt)
+            kept[c] = rot.tile([P, 2, CW], F32, name="a_sb", tag="a_sb", bufs=3)
+            nc.vector.tensor_tensor(
+                out=kept[c][:], in0=pair(gate[(U, c)], 1), in1=raw[("h", b)][:, 2:4, lo : lo + CW], op=ALU.mult
+            )
 
-        def finish_diff(c):
-            scale_diff(c, 0)
-            scale_diff(c, 1)
-            sub_store(c, 0)
-            sub_store(c, 1)
+        def scale_diff(c):
+            for t in range(2):
+                ut = gate[(U, c)][:, t, :]
+                nc.vector.tensor_tensor(out=ut, in0=ut, in1=diff[(c, t)], op=ALU.mult)
+
+        def scale_new(c):
+            nt = pair(gate[(N, c)], 1)
+            nc.vector.scalar_tensor_tensor(
+                out=nt, in0=pair(gate[(U, c)], 1), scalar=1.0, in1=nt, op0=ALU.subtract, op1=ALU.mult
+            )
+
+        def blend_diff(c):
+            nt = pair(gate[(N, c)], 0)
+            nc.vector.tensor_tensor(out=nt, in0=nt, in1=pair(gate[(U, c)], 0), op=ALU.subtract)
+            store(c, 0, nt)
+
+        def blend_sum(c):
+            nc.vector.tensor_tensor(out=kept[c][:], in0=kept[c][:], in1=pair(gate[(N, c)], 1), op=ALU.subtract)
+            store(c, 1, kept[c][:])
 
         regroup("x", 0)
         regroup("h", 0)
@@ -248,27 +247,30 @@ def tile_gru_kernel(tc, x, h, w_r, b_r, w_u, b_u, w_h, b_h, out):
         finish_weight(N)
         quantise("hr", 0)
         conv(U, 0)
+        keep_old(0)
         for c in range(1, NCHUNK):
             conv(R, c)
             if c + 1 < NCHUNK:
                 regroup("x", c + 1)
-                quantise("x", c + 1)
-            if c - 1 not in DIFF:
-                mix_a(c - 1)
-            conv(N, c - 1)
             reset(c)
+            if c + 1 < NCHUNK:
+                quantise("x", c + 1)
+            conv(N, c - 1)
             quantise("hr", c)
+            make_diff(c - 1)
             if c + 1 < NCHUNK:
                 regroup("h", c + 1)
             conv(U, c)
-            if c - 1 in DIFF:
-                make_diff(c - 1)
+            scale_new(c - 1)
+            scale_diff(c - 1)
             if c + 1 < NCHUNK:
                 quantise("h", c + 1)
-            if c - 1 in DIFF:
-                finish_diff(c - 1)
-            else:
-                mix_out(c - 1, T)
+            keep_old(c)
+            blend_sum(c - 1)
+            blend_diff(c - 1)
         conv(N, NCHUNK - 1)
         make_diff(NCHUNK - 1)
-        finish_diff(NCHUNK - 1)
+        scale_diff(NCHUNK - 1)
+        scale_new(NCHUNK - 1)
+        blend_diff(NCHUNK - 1)
+        blend_sum(NCHUNK - 1)

@@ -16,8 +16,8 @@ T = 4
 B = 2
 CH = 512
 L = 1024
+BANK = 512
 CHUNKS = ((0, 0, 512), (0, 512, 512), (1, 0, 512), (1, 512, 256), (1, 768, 256))
-LOADS = (("a", 0, 0, 1024), ("w", 0), ("w", 1), ("w", 2), ("a", 1, 0, 1024))
 NCHUNK = len(CHUNKS)
 FLOPS = 2 * 3 * CH * (2 * CH) * B * L
 
@@ -25,8 +25,8 @@ R = 0
 U = 1
 N = 2
 
-VECTOR_REGROUPS = (("x", 1), ("h", 0), ("h", 1), ("x", 2))
-W_STEP = (1, 2, 2)
+DIFF_TILES = (1, 1, 1, 2, 2)
+SHARES = {("x", 1): "V", ("h", 0): "V", ("h", 1): "V", ("x", 2): "V"}
 VECTOR_WEIGHT_COPIES = ((R, 3), (U, 0))
 
 
@@ -62,117 +62,129 @@ def tile_gru_kernel(tc, x, h, w_r, b_r, w_u, b_u, w_h, b_h, out):
         for nm in ("x", "h", "hr"):
             codes[nm] = keep.tile([P, B * L], U32, name="codes_%s" % nm, align_bytes=64)
             scales[nm] = keep.tile([P, B * L], U8, name="scales_%s" % nm, align_bytes=64)
-        bias_bf = [keep.tile([P, T], BF16, name="bias_bf%d" % g) for g in range(3)]
+        bias = [keep.tile([P, T], BF16, name="bias%d" % g) for g in range(3)]
 
         def rows(ap2d):
             return ap2d.rearrange("(u p e) l -> p u e l", u=2, p=P, e=2)
 
-        def load_act(nm, b, lo, w):
+        def load_act(nm, b):
             for u in range(2):
-                nc.sync.dma_start(
-                    out=raw[(nm, b)][:, 2 * u : 2 * u + 2, lo : lo + w], in_=rows(dram[nm][b])[:, u, :, lo : lo + w]
-                )
+                nc.sync.dma_start(out=raw[(nm, b)][:, 2 * u : 2 * u + 2, :], in_=rows(dram[nm][b])[:, u, :, :])
 
         def load_w(g):
             for u in range(2):
                 nc.sync.dma_start(out=w_sb[g][:, 2 * u : 2 * u + 2, :], in_=rows(weights[g])[:, u, :, :])
 
-        for g in range(3):
-            nc.scalar.dma_start(
-                out=bias_bf[g][:].rearrange("p (u e) -> p u e", u=2),
+        def load_bias(g):
+            nc.sync.dma_start(
+                out=bias[g][:].rearrange("p (u e) -> p u e", u=2),
                 in_=biases[g].rearrange("(u p e) -> p u e", u=2, p=P, e=2),
             )
 
-        for item in LOADS:
-            if item[0] == "w":
-                load_w(item[1])
-            else:
-                load_act("x", item[1], item[2], item[3])
-                load_act("h", item[1], item[2], item[3])
+        load_act("x", 0)
+        load_act("h", 0)
+        load_w(R)
+        for g in range(3):
+            load_bias(g)
+        load_w(U)
+        load_w(N)
+        load_act("x", 1)
+        load_act("h", 1)
 
         grp = {}
         gate = {}
-        mix = {}
+        result = {}
 
         def regroup(nm, c):
-            b, lo, CW = CHUNKS[c]
+            b, lo, w = CHUNKS[c]
             if nm == "x":
-                dst = rot.tile([P, CW, T], BF16, name="x_grp", tag="x_grp", bufs=2, align_bytes=64)
+                dst = rot.tile([P, w, T], BF16, name="x_grp", tag="x_grp", bufs=2, align_bytes=64)
             else:
-                dst = keep.tile([P, CW, T], BF16, name="h_grp%d" % c, align_bytes=64)
+                dst = keep.tile([P, w, T], BF16, name="h_grp%d" % c, align_bytes=64)
             grp[(nm, c)] = dst
-            o_ap = dst[:].rearrange("p (c i) t -> p c t i", i=4)
-            i_ap = raw[(nm, b)][:, :, lo : lo + CW].rearrange("p t (c i) -> p c t i", i=4)
-            if (nm, c) in VECTOR_REGROUPS:
-                nc.vector.tensor_copy(out=o_ap, in_=i_ap)
-            else:
-                nc.scalar.copy(out=o_ap, in_=i_ap)
+            share = SHARES.get((nm, c), "S")
+            step = w // len(share)
+            for i, who in enumerate(share):
+                o_ap = dst[:, i * step : (i + 1) * step, :].rearrange("p (c i) t -> p c t i", i=4)
+                i_ap = raw[(nm, b)][:, :, lo + i * step : lo + (i + 1) * step].rearrange("p t (c i) -> p c t i", i=4)
+                if who == "V":
+                    nc.vector.tensor_copy(out=o_ap, in_=i_ap)
+                else:
+                    nc.scalar.copy(out=o_ap, in_=i_ap)
 
         def quantise(nm, c):
-            b, lo, CW = CHUNKS[c]
+            b, lo, w = CHUNKS[c]
             g0 = b * L + lo
             nc.vector.quantize_mx(
-                out=codes[nm][:, g0 : g0 + CW].bitcast(FP8X4),
-                scales=scales[nm][:, g0 : g0 + CW],
+                out=codes[nm][:, g0 : g0 + w].bitcast(FP8X4),
+                scales=scales[nm][:, g0 : g0 + w],
                 in_=grp[(nm, c)][:].rearrange("p l t -> p (l t)"),
             )
 
         turned = {}
+        w_grp = {}
 
-        def turn_weight(g):
+        def turn_weight(g, t):
             w32 = w_sb[g][:].bitcast(F32)
-            turned[g] = []
-            for t in range(T):
-                bk = psum.tile([P, 4, P], F32, name="bank", tag="bank")
-                turned[g].append(bk)
-                for a in range(4):
-                    nc.tensor.transpose(bk[:, a, :], w32[:, t, a * P : (a + 1) * P], ident[:])
+            bank = psum.tile([P, 4, P], F32, name="bank", tag="bank")
+            turned[(g, t)] = bank
+            for a in range(4):
+                nc.tensor.transpose(bank[:, a, :], w32[:, t, a * P : (a + 1) * P], ident[:])
 
-        def finish_weight(g):
-            w_grp = rot.tile([P, T * 2 * P * 4], BF16, name="w_grp", tag="w_grp", bufs=2, align_bytes=64)
-            g32 = w_grp[:].bitcast(F32).rearrange("p (t g o u) -> p t g o u", t=T, g=2, o=P, u=2)
-            for t in range(T):
-                src = turned[g][t][:].rearrange("p (g u) o -> p g o u", g=2)
-                if (g, t) in VECTOR_WEIGHT_COPIES:
-                    nc.vector.tensor_copy(out=g32[:, t], in_=src)
-                else:
-                    nc.scalar.copy(out=g32[:, t], in_=src)
-                if t % W_STEP[g] == W_STEP[g] - 1:
-                    lo, hi = t + 1 - W_STEP[g], t + 1
-                    nc.vector.quantize_mx(
-                        out=wq[g][:, lo * 2 * P : hi * 2 * P].bitcast(FP8X4),
-                        scales=ws[g][:, lo * 2 * P : hi * 2 * P],
-                        in_=w_grp[:, lo * 8 * P : hi * 8 * P],
-                    )
+        def copy_weight(g, t):
+            if g not in w_grp:
+                w_grp[g] = rot.tile([P, T, 8 * P], BF16, name="w_grp", tag="w_grp", bufs=2, align_bytes=64)
+            dst = w_grp[g][:, t, :].bitcast(F32).rearrange("p (g o u) -> p g o u", g=2, o=P, u=2)
+            src = turned[(g, t)][:].rearrange("p (g u) o -> p g o u", g=2)
+            if (g, t) in VECTOR_WEIGHT_COPIES:
+                nc.vector.tensor_copy(out=dst, in_=src)
+            else:
+                nc.scalar.copy(out=dst, in_=src)
 
-        def conv(g, c):
-            b, lo, CW = CHUNKS[c]
+        def quantise_weight(g, t0, t1):
+            nc.vector.quantize_mx(
+                out=wq[g][:, t0 * 2 * P : t1 * 2 * P].bitcast(FP8X4),
+                scales=ws[g][:, t0 * 2 * P : t1 * 2 * P],
+                in_=w_grp[g][:, t0:t1, :].rearrange("p t n -> p (t n)"),
+            )
+
+        def conv(g, c, bufs):
+            b, lo, w = CHUNKS[c]
             g0 = b * L + lo
-            nm_tile = ("r_sb", "u_sb", "n_sb")[g]
-            dst = rot.tile([P, T, CW], F32, name=nm_tile, tag=nm_tile, bufs=(2, 3, 2)[g])
-            gate[(g, c)] = dst
+            d = DIFF_TILES[c]
+            if g == N:
+                new = rot.tile([P, T, w], F32, name="m_sb", tag="m_sb", bufs=2)
+                gate[(N, c)] = new
+            else:
+                nm_tile = ("r_sb", "u_sb")[g]
+                gate[(g, c)] = rot.tile([P, T, w], F32, name=nm_tile, tag=nm_tile, bufs=bufs)
+            if g == U:
+                result[c] = rot.tile([P, T, w], F32, name="a_sb", tag="a_sb", bufs=3)
             banks = []
-            for k in range(2):
-                nm = "x" if k == 0 else ("hr" if g == N else "h")
-                for t in range(T):
-                    if k == 0:
-                        banks.append(psum.tile([P, 512], F32, name="bank", tag="bank"))
-                    wsl = slice((t * 2 + k) * P, (t * 2 + k + 1) * P)
-                    nc.tensor.matmul_mx(
-                        out=banks[t][:, 0:CW],
-                        lhsT=wq[g][:, wsl].bitcast(FP8X4),
-                        lhsT_scale=ws[g][:, wsl],
-                        rhs=codes[nm][:, g0 : g0 + CW].bitcast(FP8X4),
-                        rhs_scale=scales[nm][:, g0 : g0 + CW],
-                        start=(k == 0),
-                        stop=(k == 1),
-                    )
             for t in range(T):
-                nc.scalar.activation(out=dst[:, t, :], in_=banks[t][:, 0:CW], func=funcs[g], bias=bias_bf[g][:, t : t + 1], scale=1.0)
+                banks.append(psum.tile([P, BANK], F32, name="bank", tag="bank"))
+            order = [(k, t) for k in range(2) for t in range(T)] if False else [(k, t) for t in range(T) for k in range(2)]
+            for k, t in order:
+                nm = "x" if k == 0 else ("hr" if g == N else "h")
+                wsl = slice((t * 2 + k) * P, (t * 2 + k + 1) * P)
+                nc.tensor.matmul_mx(
+                    out=banks[t][:, 0:w],
+                    lhsT=wq[g][:, wsl].bitcast(FP8X4),
+                    lhsT_scale=ws[g][:, wsl],
+                    rhs=codes[nm][:, g0 : g0 + w].bitcast(FP8X4),
+                    rhs_scale=scales[nm][:, g0 : g0 + w],
+                    start=(k == 0),
+                    stop=(k == 1),
+                )
+            for t in range(T):
+                dst = result[c] if g == N and t < d else gate[(g, c)]
+                nc.scalar.activation(
+                    out=dst[:, t, :], in_=banks[t][:, 0:w], func=funcs[g], bias=bias[g][:, t : t + 1], scale=1.0
+                )
 
         def reset(c):
-            b, lo, CW = CHUNKS[c]
-            dst = rot.tile([P, CW, T], BF16, name="hr_grp", tag="hr_grp", bufs=2, align_bytes=64)
+            b, lo, w = CHUNKS[c]
+            dst = rot.tile([P, w, T], BF16, name="hr_grp", tag="hr_grp", bufs=2, align_bytes=64)
             grp[("hr", c)] = dst
             nc.vector.tensor_tensor(
                 out=dst[:].rearrange("p (c i) t -> p c t i", i=4),
@@ -181,96 +193,104 @@ def tile_gru_kernel(tc, x, h, w_r, b_r, w_u, b_u, w_h, b_h, out):
                 op=ALU.mult,
             )
 
-        kept = {}
         diff = {}
 
-        def pair(tile, u):
-            return tile[:, 2 * u : 2 * u + 2, :]
-
-        def store(c, u, tile):
-            b, lo, CW = CHUNKS[c]
-            nc.sync.dma_start(out=rows(out[b])[:, u, :, lo : lo + CW], in_=tile)
-
         def make_diff(c):
-            b, lo, CW = CHUNKS[c]
-            for t in range(2):
-                if t == 0 or CW == 512:
-                    bank = psum.tile([P, 512 // CW, CW], F32, name="bank", tag="bank")
-                diff[(c, t)] = bank[:, t % (512 // CW), :]
-                nc.tensor.matmul(
-                    diff[(c, t)], lhsT=minus[:], rhs=raw[("h", b)][:, t, lo : lo + CW], start=True, stop=False
-                )
-                nc.tensor.matmul(diff[(c, t)], lhsT=ident[:], rhs=gate[(N, c)][:, t, :], start=False, stop=True)
-
-        def keep_old(c):
-            b, lo, CW = CHUNKS[c]
-            kept[c] = rot.tile([P, 2, CW], F32, name="a_sb", tag="a_sb", bufs=3)
-            nc.vector.tensor_tensor(
-                out=kept[c][:], in0=pair(gate[(U, c)], 1), in1=raw[("h", b)][:, 2:4, lo : lo + CW], op=ALU.mult
-            )
+            b, lo, w = CHUNKS[c]
+            for t in range(DIFF_TILES[c]):
+                if (t * w) % BANK == 0:
+                    bank = psum.tile([P, BANK // w, w], F32, name="bank", tag="bank")
+                d_ap = bank[:, t % (BANK // w), :]
+                if (t * w) % BANK == 0:
+                    diff[(c, t)] = bank
+                nc.tensor.matmul(d_ap, lhsT=minus[:], rhs=raw[("h", b)][:, t, lo : lo + w], start=True, stop=False)
+                nc.tensor.matmul(d_ap, lhsT=ident[:], rhs=result[c][:, t, :], start=False, stop=True)
 
         def scale_diff(c):
-            for t in range(2):
-                ut = gate[(U, c)][:, t, :]
-                nc.vector.tensor_tensor(out=ut, in0=ut, in1=diff[(c, t)], op=ALU.mult)
+            b, lo, w = CHUNKS[c]
+            step = BANK // w
+            for t in range(0, DIFF_TILES[c], step):
+                n = min(step, DIFF_TILES[c] - t)
+                ut = gate[(U, c)][:, t : t + n, :]
+                nc.vector.tensor_tensor(out=ut, in0=ut, in1=diff[(c, t)][:, 0:n, :], op=ALU.mult)
+
+        def keep_old(c):
+            b, lo, w = CHUNKS[c]
+            d = DIFF_TILES[c]
+            if d < T:
+                nc.vector.tensor_tensor(
+                    out=result[c][:, d:T, :], in0=gate[(U, c)][:, d:T, :], in1=raw[("h", b)][:, d:T, lo : lo + w], op=ALU.mult
+                )
 
         def scale_new(c):
-            nt = pair(gate[(N, c)], 1)
-            nc.vector.scalar_tensor_tensor(
-                out=nt, in0=pair(gate[(U, c)], 1), scalar=1.0, in1=nt, op0=ALU.subtract, op1=ALU.mult
-            )
+            d = DIFF_TILES[c]
+            if d < T:
+                ut = gate[(U, c)][:, d:T, :]
+                nc.vector.scalar_tensor_tensor(
+                    out=ut, in0=ut, scalar=1.0, in1=gate[(N, c)][:, d:T, :], op0=ALU.subtract, op1=ALU.mult
+                )
 
-        def blend_diff(c):
-            nt = pair(gate[(N, c)], 0)
-            nc.vector.tensor_tensor(out=nt, in0=nt, in1=pair(gate[(U, c)], 0), op=ALU.subtract)
-            store(c, 0, nt)
-
-        def blend_sum(c):
-            nc.vector.tensor_tensor(out=kept[c][:], in0=kept[c][:], in1=pair(gate[(N, c)], 1), op=ALU.subtract)
-            store(c, 1, kept[c][:])
+        def blend(c, step):
+            b, lo, w = CHUNKS[c]
+            for t in range(0, T, step):
+                rt = result[c][:, t : t + step, :]
+                nc.vector.tensor_tensor(out=rt, in0=rt, in1=gate[(U, c)][:, t : t + step, :], op=ALU.subtract)
+                for u in range(t // 2, (t + step) // 2):
+                    nc.sync.dma_start(
+                        out=rows(out[b])[:, u, :, lo : lo + w], in_=result[c][:, 2 * u : 2 * u + 2, :]
+                    )
 
         regroup("x", 0)
-        regroup("h", 0)
         quantise("x", 0)
+        regroup("h", 0)
         quantise("h", 0)
-        turn_weight(R)
-        finish_weight(R)
+        for t in range(T):
+            turn_weight(R, t)
+        for t in range(T):
+            copy_weight(R, t)
+            quantise_weight(R, t, t + 1)
         regroup("x", 1)
         regroup("h", 1)
         quantise("h", 1)
         quantise("x", 1)
-        turn_weight(U)
-        conv(R, 0)
-        finish_weight(U)
+        for t in range(T):
+            turn_weight(U, t)
+        conv(R, 0, 2)
+        for t in range(T):
+            copy_weight(U, t)
+            if t % 2 == 1:
+                quantise_weight(U, t - 1, t + 1)
         reset(0)
-        turn_weight(N)
-        finish_weight(N)
+        for t in range(T):
+            turn_weight(N, t)
+        for t in range(T):
+            copy_weight(N, t)
+            if t % 2 == 1:
+                quantise_weight(N, t - 1, t + 1)
         quantise("hr", 0)
-        conv(U, 0)
+        conv(U, 0, 3)
         keep_old(0)
         for c in range(1, NCHUNK):
-            conv(R, c)
+            conv(R, c, 2)
             if c + 1 < NCHUNK:
                 regroup("x", c + 1)
             reset(c)
             if c + 1 < NCHUNK:
                 quantise("x", c + 1)
-            conv(N, c - 1)
+            conv(N, c - 1, 2)
             quantise("hr", c)
             make_diff(c - 1)
             if c + 1 < NCHUNK:
                 regroup("h", c + 1)
-            conv(U, c)
+            conv(U, c, 3)
             scale_new(c - 1)
             scale_diff(c - 1)
             if c + 1 < NCHUNK:
                 quantise("h", c + 1)
             keep_old(c)
-            blend_sum(c - 1)
-            blend_diff(c - 1)
-        conv(N, NCHUNK - 1)
+            blend(c - 1, T)
+        conv(N, NCHUNK - 1, 2)
         make_diff(NCHUNK - 1)
         scale_diff(NCHUNK - 1)
         scale_new(NCHUNK - 1)
-        blend_diff(NCHUNK - 1)
-        blend_sum(NCHUNK - 1)
+        blend(NCHUNK - 1, 2)

@@ -26,8 +26,8 @@ U = 1
 N = 2
 
 DIFF_TILES = (1, 1, 1, 2, 2)
-SHARES = {("x", 1): "V", ("h", 0): "V", ("h", 1): "V", ("x", 2): "V"}
-VECTOR_WEIGHT_COPIES = ((R, 3), (U, 0))
+SHARES = {("x", 0): "V", ("h", 0): "V", ("x", 1): "V", ("h", 1): "VS", ("x", 2): "V"}
+VECTOR_WEIGHT_COPIES = ((R, 3),)
 
 
 def tile_gru_kernel(tc, x, h, w_r, b_r, w_u, b_u, w_h, b_h, out):
@@ -50,26 +50,31 @@ def tile_gru_kernel(tc, x, h, w_r, b_r, w_u, b_u, w_h, b_h, out):
         nc.gpsimd.tensor_scalar(out=minus[:], in0=ident[:], scalar1=-1.0, scalar2=0.0, op0=ALU.mult, op1=ALU.add)
 
         raw = {}
-        for nm in ("x", "h"):
-            for b in range(B):
-                raw[(nm, b)] = keep.tile([P, T, L], BF16, name="raw_%s%d" % (nm, b))
         dram = {"x": x, "h": h}
         w_sb = [keep.tile([P, T, 2 * CH], BF16, name="w_sb%d" % g) for g in range(3)]
         wq = [keep.tile([P, T * 2 * P], U32, name="wq%d" % g, align_bytes=64) for g in range(3)]
         ws = [keep.tile([P, T * 2 * P], U8, name="ws%d" % g, align_bytes=64) for g in range(3)]
         codes = {}
         scales = {}
-        for nm in ("x", "h", "hr"):
-            codes[nm] = keep.tile([P, B * L], U32, name="codes_%s" % nm, align_bytes=64)
-            scales[nm] = keep.tile([P, B * L], U8, name="scales_%s" % nm, align_bytes=64)
+        for nm in ("xh", "hr"):
+            n = 2 * B * L if nm == "xh" else B * L
+            codes[nm] = keep.tile([P, n], U32, name="codes_%s" % nm, align_bytes=64)
+            scales[nm] = keep.tile([P, n], U8, name="scales_%s" % nm, align_bytes=64)
         bias = [keep.tile([P, T], BF16, name="bias%d" % g) for g in range(3)]
 
         def rows(ap2d):
             return ap2d.rearrange("(u p e) l -> p u e l", u=2, p=P, e=2)
 
-        def load_act(nm, b):
+        def load_act(nm, b, lo=0, w=L):
+            tile = keep.tile([P, T, w], BF16, name="raw_%s%d_%d" % (nm, b, lo))
+            for c in range(NCHUNK):
+                cb, clo, cw = CHUNKS[c]
+                if cb == b and lo <= clo < lo + w:
+                    raw[(nm, c)] = tile[:, :, clo - lo : clo - lo + cw]
             for u in range(2):
-                nc.sync.dma_start(out=raw[(nm, b)][:, 2 * u : 2 * u + 2, :], in_=rows(dram[nm][b])[:, u, :, :])
+                nc.sync.dma_start(
+                    out=tile[:, 2 * u : 2 * u + 2, :], in_=rows(dram[nm][b])[:, u, :, lo : lo + w]
+                )
 
         def load_w(g):
             for u in range(2):
@@ -81,15 +86,17 @@ def tile_gru_kernel(tc, x, h, w_r, b_r, w_u, b_u, w_h, b_h, out):
                 in_=biases[g].rearrange("(u p e) -> p u e", u=2, p=P, e=2),
             )
 
-        load_act("x", 0)
-        load_act("h", 0)
+        load_act("x", 0, 0, 512)
+        load_act("h", 0, 0, 512)
         load_w(R)
         for g in range(3):
             load_bias(g)
+        load_act("x", 0, 512, 512)
+        load_act("h", 0, 512, 512)
         load_w(U)
         load_w(N)
-        load_act("x", 1)
-        load_act("h", 1)
+        load_act("x", 1, 0, 1024)
+        load_act("h", 1, 0, 1024)
 
         grp = {}
         gate = {}
@@ -97,28 +104,39 @@ def tile_gru_kernel(tc, x, h, w_r, b_r, w_u, b_u, w_h, b_h, out):
 
         def regroup(nm, c):
             b, lo, w = CHUNKS[c]
-            if nm == "x":
-                dst = rot.tile([P, w, T], BF16, name="x_grp", tag="x_grp", bufs=2, align_bytes=64)
-            else:
-                dst = keep.tile([P, w, T], BF16, name="h_grp%d" % c, align_bytes=64)
-            grp[(nm, c)] = dst
+            if c not in grp:
+                grp[c] = keep.tile([P, 2, w, T], BF16, name="grp%d" % c, align_bytes=64)
+            dst = grp[c][:, 0 if nm == "x" else 1, :, :]
             share = SHARES.get((nm, c), "S")
             step = w // len(share)
             for i, who in enumerate(share):
                 o_ap = dst[:, i * step : (i + 1) * step, :].rearrange("p (c i) t -> p c t i", i=4)
-                i_ap = raw[(nm, b)][:, :, lo + i * step : lo + (i + 1) * step].rearrange("p t (c i) -> p c t i", i=4)
+                i_ap = raw[(nm, c)][:, :, i * step : (i + 1) * step].rearrange("p t (c i) -> p c t i", i=4)
                 if who == "V":
                     nc.vector.tensor_copy(out=o_ap, in_=i_ap)
                 else:
                     nc.scalar.copy(out=o_ap, in_=i_ap)
 
-        def quantise(nm, c):
+        def operand(nm, c):
             b, lo, w = CHUNKS[c]
             g0 = b * L + lo
+            if nm == "hr":
+                return "hr", g0
+            return "xh", 2 * g0 + (0 if nm == "x" else w)
+
+        def quantise(nm, c):
+            b, lo, w = CHUNKS[c]
+            if nm == "xh":
+                key, g0 = operand("x", c)
+                n = 2 * w
+                src = grp[c][:].rearrange("p s l t -> p (s l t)")
+            else:
+                key, g0 = operand(nm, c)
+                n = w
+                src = grp[("hr", c)][:] if nm == "hr" else grp[c][:, 0 if nm == "x" else 1, :, :]
+                src = src.rearrange("p l t -> p (l t)")
             nc.vector.quantize_mx(
-                out=codes[nm][:, g0 : g0 + w].bitcast(FP8X4),
-                scales=scales[nm][:, g0 : g0 + w],
-                in_=grp[(nm, c)][:].rearrange("p l t -> p (l t)"),
+                out=codes[key][:, g0 : g0 + n].bitcast(FP8X4), scales=scales[key][:, g0 : g0 + n], in_=src
             )
 
         turned = {}
@@ -150,7 +168,6 @@ def tile_gru_kernel(tc, x, h, w_r, b_r, w_u, b_u, w_h, b_h, out):
 
         def conv(g, c, bufs):
             b, lo, w = CHUNKS[c]
-            g0 = b * L + lo
             d = DIFF_TILES[c]
             if g == N:
                 new = rot.tile([P, T, w], F32, name="m_sb", tag="m_sb", bufs=2)
@@ -165,14 +182,14 @@ def tile_gru_kernel(tc, x, h, w_r, b_r, w_u, b_u, w_h, b_h, out):
                 banks.append(psum.tile([P, BANK], F32, name="bank", tag="bank"))
             order = [(k, t) for k in range(2) for t in range(T)] if False else [(k, t) for t in range(T) for k in range(2)]
             for k, t in order:
-                nm = "x" if k == 0 else ("hr" if g == N else "h")
+                key, g0 = operand("x" if k == 0 else ("hr" if g == N else "h"), c)
                 wsl = slice((t * 2 + k) * P, (t * 2 + k + 1) * P)
                 nc.tensor.matmul_mx(
                     out=banks[t][:, 0:w],
                     lhsT=wq[g][:, wsl].bitcast(FP8X4),
                     lhsT_scale=ws[g][:, wsl],
-                    rhs=codes[nm][:, g0 : g0 + w].bitcast(FP8X4),
-                    rhs_scale=scales[nm][:, g0 : g0 + w],
+                    rhs=codes[key][:, g0 : g0 + w].bitcast(FP8X4),
+                    rhs_scale=scales[key][:, g0 : g0 + w],
                     start=(k == 0),
                     stop=(k == 1),
                 )
@@ -188,7 +205,7 @@ def tile_gru_kernel(tc, x, h, w_r, b_r, w_u, b_u, w_h, b_h, out):
             grp[("hr", c)] = dst
             nc.vector.tensor_tensor(
                 out=dst[:].rearrange("p (c i) t -> p c t i", i=4),
-                in0=grp[("h", c)][:].rearrange("p (c i) t -> p c t i", i=4),
+                in0=grp[c][:, 1, :, :].rearrange("p (c i) t -> p c t i", i=4),
                 in1=gate[(R, c)][:].rearrange("p t (c i) -> p c t i", i=4),
                 op=ALU.mult,
             )
@@ -203,7 +220,7 @@ def tile_gru_kernel(tc, x, h, w_r, b_r, w_u, b_u, w_h, b_h, out):
                 d_ap = bank[:, t % (BANK // w), :]
                 if (t * w) % BANK == 0:
                     diff[(c, t)] = bank
-                nc.tensor.matmul(d_ap, lhsT=minus[:], rhs=raw[("h", b)][:, t, lo : lo + w], start=True, stop=False)
+                nc.tensor.matmul(d_ap, lhsT=minus[:], rhs=raw[("h", c)][:, t, :], start=True, stop=False)
                 nc.tensor.matmul(d_ap, lhsT=ident[:], rhs=result[c][:, t, :], start=False, stop=True)
 
         def scale_diff(c):
@@ -219,7 +236,7 @@ def tile_gru_kernel(tc, x, h, w_r, b_r, w_u, b_u, w_h, b_h, out):
             d = DIFF_TILES[c]
             if d < T:
                 nc.vector.tensor_tensor(
-                    out=result[c][:, d:T, :], in0=gate[(U, c)][:, d:T, :], in1=raw[("h", b)][:, d:T, lo : lo + w], op=ALU.mult
+                    out=result[c][:, d:T, :], in0=gate[(U, c)][:, d:T, :], in1=raw[("h", c)][:, d:T, :], op=ALU.mult
                 )
 
         def scale_new(c):

@@ -25,8 +25,8 @@ R = 0
 U = 1
 N = 2
 
-DIFF_TILES = (1, 1, 1, 2, 2)
-SHARES = {("x", 0): "V", ("h", 0): "V", ("x", 1): "V", ("h", 1): "VS", ("x", 2): "V"}
+DIFF_TILES = (1, 2, 1, 2, 2)
+SHARES = {("x", 0): "V", ("h", 0): "VS", ("x", 1): "V", ("h", 1): "V", ("x", 2): "V"}
 VECTOR_WEIGHT_COPIES = ((R, 3),)
 
 
@@ -257,57 +257,66 @@ def tile_gru_kernel(tc, x, h, w_r, b_r, w_u, b_u, w_h, b_h, out):
                         out=rows(out[b])[:, u, :, lo : lo + w], in_=result[c][:, 2 * u : 2 * u + 2, :]
                     )
 
-        regroup("x", 0)
-        quantise("x", 0)
-        regroup("h", 0)
-        quantise("h", 0)
-        for t in range(T):
-            turn_weight(R, t)
-        for t in range(T):
-            copy_weight(R, t)
-            quantise_weight(R, t, t + 1)
-        regroup("x", 1)
-        regroup("h", 1)
-        quantise("h", 1)
-        quantise("x", 1)
-        for t in range(T):
-            turn_weight(U, t)
-        conv(R, 0, 2)
-        for t in range(T):
-            copy_weight(U, t)
-            if t % 2 == 1:
-                quantise_weight(U, t - 1, t + 1)
-        reset(0)
-        for t in range(T):
-            turn_weight(N, t)
-        for t in range(T):
-            copy_weight(N, t)
-            if t % 2 == 1:
-                quantise_weight(N, t - 1, t + 1)
-        quantise("hr", 0)
-        conv(U, 0, 3)
-        keep_old(0)
-        for c in range(1, NCHUNK):
-            conv(R, c, 2)
-            if c + 1 < NCHUNK:
-                regroup("x", c + 1)
-            reset(c)
-            if c + 1 < NCHUNK:
-                quantise("x", c + 1)
-            conv(N, c - 1, 2)
-            quantise("hr", c)
-            make_diff(c - 1)
-            if c + 1 < NCHUNK:
-                regroup("h", c + 1)
-            conv(U, c, 3)
-            scale_new(c - 1)
-            scale_diff(c - 1)
-            if c + 1 < NCHUNK:
-                quantise("h", c + 1)
-            keep_old(c)
-            blend(c - 1, T)
-        conv(N, NCHUNK - 1, 2)
-        make_diff(NCHUNK - 1)
-        scale_diff(NCHUNK - 1)
-        scale_new(NCHUNK - 1)
-        blend(NCHUNK - 1, 2)
+        with tc.manual_schedule(engines={mybir.EngineType.DVE, mybir.EngineType.Activation, mybir.EngineType.PE}):
+            regroup("x", 0)
+            quantise("x", 0)
+            regroup("h", 0)
+            quantise("h", 0)
+            for t in range(T):
+                turn_weight(R, t)
+            copy_weight(R, 0)
+            quantise_weight(R, 0, 1)
+            copy_weight(R, 1)
+            quantise_weight(R, 1, 2)
+            copy_weight(R, 2)
+            copy_weight(R, 3)
+            quantise_weight(R, 2, 3)
+            quantise_weight(R, 3, 4)
+            conv(R, 0, 2)
+            regroup("x", 1)
+            regroup("h", 1)
+            quantise("x", 1)
+            quantise("h", 1)
+            for t in range(T):
+                turn_weight(U, t)
+            for t in range(T):
+                copy_weight(U, t)
+            quantise_weight(U, 0, 2)
+            reset(0)
+            quantise_weight(U, 2, 4)
+            conv(R, 1, 2)
+            for t in range(T):
+                turn_weight(N, t)
+            for t in range(T):
+                copy_weight(N, t)
+            quantise("hr", 0)
+            regroup("x", 2)
+            quantise_weight(N, 0, 2)
+            quantise_weight(N, 2, 4)
+            conv(U, 0, 3)
+            for c in range(1, NCHUNK):
+                if c > 1:
+                    conv(R, c, 2)
+                if 2 < c + 1 < NCHUNK:
+                    regroup("x", c + 1)
+                reset(c)
+                keep_old(c - 1)
+                if c + 1 < NCHUNK:
+                    quantise("x", c + 1)
+                conv(N, c - 1, 2)
+                quantise("hr", c)
+                make_diff(c - 1)
+                if c + 1 < NCHUNK:
+                    regroup("h", c + 1)
+                scale_new(c - 1)
+                if c + 1 < NCHUNK:
+                    quantise("h", c + 1)
+                scale_diff(c - 1)
+                conv(U, c, 3)
+                blend(c - 1, T)
+            keep_old(NCHUNK - 1)
+            conv(N, NCHUNK - 1, 2)
+            make_diff(NCHUNK - 1)
+            scale_new(NCHUNK - 1)
+            scale_diff(NCHUNK - 1)
+            blend(NCHUNK - 1, 2)

from contextlib import ExitStack

import concourse.mybir as mybir
from concourse.masks import make_identity

F32 = mybir.dt.float32
BF16 = mybir.dt.bfloat16
U32 = mybir.dt.uint32
U8 = mybir.dt.uint8
FP8X4 = mybir.dt.float8_e4m3fn_x4
ACT = mybir.ActivationFunctionType
ALU = mybir.AluOpType

P = 128
T = 4
B = 2
CH = 512
L = 1024
BANK = 512
CHUNKS = ((0, 0, 512), (0, 512, 512), (1, 0, 512), (1, 512, 256), (1, 768, 256))
NCHUNK = len(CHUNKS)
FLOPS = 2 * 3 * CH * (2 * CH) * B * L

R = 0
U = 1
N = 2

DIFF_TILES = (1, 2, 1, 2, 2)
SHARES = {("x", 0): "V", ("h", 0): "VS", ("x", 1): "V", ("h", 1): "V", ("x", 2): "V"}
VECTOR_WEIGHT_COPIES = ((R, 3),)


def tile_gru_kernel(tc, x, h, w_r, b_r, w_u, b_u, w_h, b_h, out):
    nc = tc.nc
    weights = [w_r, w_u, w_h]
    biases = [b_r, b_u, b_h]
    funcs = [ACT.Sigmoid, ACT.Sigmoid, ACT.Tanh]
    with ExitStack() as ctx:
        keep = ctx.enter_context(tc.tile_pool(name="keep", bufs=1))
        rot = ctx.enter_context(tc.tile_pool(name="rot", bufs=2))
        psum = ctx.enter_context(tc.psum_pool(name="psum", bufs=8))

        warm = keep.tile([P, 1], F32, name="warm")
        warm_out = keep.tile([P, 1], F32, name="warm_out")
        nc.vector.memset(warm[:], 0.0)
        nc.scalar.activation(out=warm_out[:], in_=warm[:], func=ACT.Sigmoid)
        ident = keep.tile([P, P], F32, name="ident")
        make_identity(nc, ident[:])
        minus = keep.tile([P, P], BF16, name="minus")
        nc.gpsimd.tensor_scalar(out=minus[:], in0=ident[:], scalar1=-1.0, scalar2=0.0, op0=ALU.mult, op1=ALU.add)

        raw = {}
        dram = {"x": x, "h": h}
        w_sb = [keep.tile([P, T, 2 * CH], BF16, name="w_sb%d" % g) for g in range(3)]
        wq = [keep.tile([P, T * 2 * P], U32, name="wq%d" % g, align_bytes=64) for g in range(3)]
        ws = [keep.tile([P, T * 2 * P], U8, name="ws%d" % g, align_bytes=64) for g in range(3)]
        codes = {}
        scales = {}
        for nm in ("xh", "hr"):
            n = 2 * B * L if nm == "xh" else B * L
            codes[nm] = keep.tile([P, n], U32, name="codes_%s" % nm, align_bytes=64)
            scales[nm] = keep.tile([P, n], U8, name="scales_%s" % nm, align_bytes=64)
        bias = [keep.tile([P, T], BF16, name="bias%d" % g) for g in range(3)]

        def rows(ap2d):
            return ap2d.rearrange("(u p e) l -> p u e l", u=2, p=P, e=2)

        def load_act(nm, b, lo=0, w=L):
            tile = keep.tile([P, T, w], BF16, name="raw_%s%d_%d" % (nm, b, lo))
            for c in range(NCHUNK):
                cb, clo, cw = CHUNKS[c]
                if cb == b and lo <= clo < lo + w:
                    raw[(nm, c)] = tile[:, :, clo - lo : clo - lo + cw]
            for u in range(2):
                nc.sync.dma_start(
                    out=tile[:, 2 * u : 2 * u + 2, :], in_=rows(dram[nm][b])[:, u, :, lo : lo + w]
                )

        def load_w(g):
            for u in range(2):
                nc.sync.dma_start(out=w_sb[g][:, 2 * u : 2 * u + 2, :], in_=rows(weights[g])[:, u, :, :])

        def load_bias(g):
            nc.sync.dma_start(
                out=bias[g][:].rearrange("p (u e) -> p u e", u=2),
                in_=biases[g].rearrange("(u p e) -> p u e", u=2, p=P, e=2),
            )

        load_act("x", 0, 0, 512)
        load_act("h", 0, 0, 512)
        load_w(R)
        for g in range(3):
            load_bias(g)
        load_act("x", 0, 512, 512)
        load_act("h", 0, 512, 512)
        load_w(U)
        load_w(N)
        load_act("x", 1, 0, 1024)
        load_act("h", 1, 0, 1024)

        grp = {}
        gate = {}
        result = {}

        def regroup(nm, c):
            b, lo, w = CHUNKS[c]
            if c not in grp:
                grp[c] = keep.tile([P, 2, w, T], BF16, name="grp%d" % c, align_bytes=64)
            dst = grp[c][:, 0 if nm == "x" else 1, :, :]
            share = SHARES.get((nm, c), "S")
            step = w // len(share)
            for i, who in enumerate(share):
                o_ap = dst[:, i * step : (i + 1) * step, :].rearrange("p (c i) t -> p c t i", i=4)
                i_ap = raw[(nm, c)][:, :, i * step : (i + 1) * step].rearrange("p t (c i) -> p c t i", i=4)
                if who == "V":
                    nc.vector.tensor_copy(out=o_ap, in_=i_ap)
                else:
                    nc.scalar.copy(out=o_ap, in_=i_ap)

        def operand(nm, c):
            b, lo, w = CHUNKS[c]
            g0 = b * L + lo
            if nm == "hr":
                return "hr", g0
            return "xh", 2 * g0 + (0 if nm == "x" else w)

        def quantise(nm, c):
            b, lo, w = CHUNKS[c]
            if nm == "xh":
                key, g0 = operand("x", c)
                n = 2 * w
                src = grp[c][:].rearrange("p s l t -> p (s l t)")
            else:
                key, g0 = operand(nm, c)
                n = w
                src = grp[("hr", c)][:] if nm == "hr" else grp[c][:, 0 if nm == "x" else 1, :, :]
                src = src.rearrange("p l t -> p (l t)")
            nc.vector.quantize_mx(
                out=codes[key][:, g0 : g0 + n].bitcast(FP8X4), scales=scales[key][:, g0 : g0 + n], in_=src
            )

        turned = {}
        w_grp = {}

        def turn_weight(g, t):
            w32 = w_sb[g][:].bitcast(F32)
            bank = psum.tile([P, 4, P], F32, name="bank", tag="bank")
            turned[(g, t)] = bank
            for a in range(4):
                nc.tensor.transpose(bank[:, a, :], w32[:, t, a * P : (a + 1) * P], ident[:])

        def copy_weight(g, t):
            if g not in w_grp:
                w_grp[g] = rot.tile([P, T, 8 * P], BF16, name="w_grp", tag="w_grp", bufs=2, align_bytes=64)
            dst = w_grp[g][:, t, :].bitcast(F32).rearrange("p (g o u) -> p g o u", g=2, o=P, u=2)
            src = turned[(g, t)][:].rearrange("p (g u) o -> p g o u", g=2)
            if (g, t) in VECTOR_WEIGHT_COPIES:
                nc.vector.tensor_copy(out=dst, in_=src)
            else:
                nc.scalar.copy(out=dst, in_=src)

        def quantise_weight(g, t0, t1):
            nc.vector.quantize_mx(
                out=wq[g][:, t0 * 2 * P : t1 * 2 * P].bitcast(FP8X4),
                scales=ws[g][:, t0 * 2 * P : t1 * 2 * P],
                in_=w_grp[g][:, t0:t1, :].rearrange("p t n -> p (t n)"),
            )

        def conv(g, c, bufs):
            b, lo, w = CHUNKS[c]
            d = DIFF_TILES[c]
            if g == N:
                new = rot.tile([P, T, w], F32, name="m_sb", tag="m_sb", bufs=2)
                gate[(N, c)] = new
            else:
                nm_tile = ("r_sb", "u_sb")[g]
                gate[(g, c)] = rot.tile([P, T, w], F32, name=nm_tile, tag=nm_tile, bufs=bufs)
            if g == U:
                result[c] = rot.tile([P, T, w], F32, name="a_sb", tag="a_sb", bufs=3)
            banks = []
            for t in range(T):
                banks.append(psum.tile([P, BANK], F32, name="bank", tag="bank"))
            order = [(k, t) for k in range(2) for t in range(T)] if False else [(k, t) for t in range(T) for k in range(2)]
            for k, t in order:
                key, g0 = operand("x" if k == 0 else ("hr" if g == N else "h"), c)
                wsl = slice((t * 2 + k) * P, (t * 2 + k + 1) * P)
                nc.tensor.matmul_mx(
                    out=banks[t][:, 0:w],
                    lhsT=wq[g][:, wsl].bitcast(FP8X4),
                    lhsT_scale=ws[g][:, wsl],
                    rhs=codes[key][:, g0 : g0 + w].bitcast(FP8X4),
                    rhs_scale=scales[key][:, g0 : g0 + w],
                    start=(k == 0),
                    stop=(k == 1),
                )
            for t in range(T):
                dst = result[c] if g == N and t < d else gate[(g, c)]
                nc.scalar.activation(
                    out=dst[:, t, :], in_=banks[t][:, 0:w], func=funcs[g], bias=bias[g][:, t : t + 1], scale=1.0
                )

        def reset(c):
            b, lo, w = CHUNKS[c]
            dst = rot.tile([P, w, T], BF16, name="hr_grp", tag="hr_grp", bufs=2, align_bytes=64)
            grp[("hr", c)] = dst
            nc.vector.tensor_tensor(
                out=dst[:].rearrange("p (c i) t -> p c t i", i=4),
                in0=grp[c][:, 1, :, :].rearrange("p (c i) t -> p c t i", i=4),
                in1=gate[(R, c)][:].rearrange("p t (c i) -> p c t i", i=4),
                op=ALU.mult,
            )

        diff = {}

        def make_diff(c):
            b, lo, w = CHUNKS[c]
            for t in range(DIFF_TILES[c]):
                if (t * w) % BANK == 0:
                    bank = psum.tile([P, BANK // w, w], F32, name="bank", tag="bank")
                d_ap = bank[:, t % (BANK // w), :]
                if (t * w) % BANK == 0:
                    diff[(c, t)] = bank
                nc.tensor.matmul(d_ap, lhsT=minus[:], rhs=raw[("h", c)][:, t, :], start=True, stop=False)
                nc.tensor.matmul(d_ap, lhsT=ident[:], rhs=result[c][:, t, :], start=False, stop=True)

        def scale_diff(c):
            b, lo, w = CHUNKS[c]
            step = BANK // w
            for t in range(0, DIFF_TILES[c], step):
                n = min(step, DIFF_TILES[c] - t)
                ut = gate[(U, c)][:, t : t + n, :]
                nc.vector.tensor_tensor(out=ut, in0=ut, in1=diff[(c, t)][:, 0:n, :], op=ALU.mult)

        def keep_old(c):
            b, lo, w = CHUNKS[c]
            d = DIFF_TILES[c]
            if d < T:
                nc.vector.tensor_tensor(
                    out=result[c][:, d:T, :], in0=gate[(U, c)][:, d:T, :], in1=raw[("h", c)][:, d:T, :], op=ALU.mult
                )

        def scale_new(c):
            d = DIFF_TILES[c]
            if d < T:
                ut = gate[(U, c)][:, d:T, :]
                nc.vector.scalar_tensor_tensor(
                    out=ut, in0=ut, scalar=1.0, in1=gate[(N, c)][:, d:T, :], op0=ALU.subtract, op1=ALU.mult
                )

        def blend(c, step):
            b, lo, w = CHUNKS[c]
            for t in range(0, T, step):
                rt = result[c][:, t : t + step, :]
                nc.vector.tensor_tensor(out=rt, in0=rt, in1=gate[(U, c)][:, t : t + step, :], op=ALU.subtract)
                for u in range(t // 2, (t + step) // 2):
                    nc.sync.dma_start(
                        out=rows(out[b])[:, u, :, lo : lo + w], in_=result[c][:, 2 * u : 2 * u + 2, :]
                    )

        with tc.manual_schedule(engines={mybir.EngineType.DVE, mybir.EngineType.Activation, mybir.EngineType.PE}):
            regroup("x", 0)
            quantise("x", 0)
            regroup("h", 0)
            quantise("h", 0)
            for t in range(T):
                turn_weight(R, t)
            copy_weight(R, 0)
            quantise_weight(R, 0, 1)
            copy_weight(R, 1)
            quantise_weight(R, 1, 2)
            copy_weight(R, 2)
            copy_weight(R, 3)
            quantise_weight(R, 2, 3)
            quantise_weight(R, 3, 4)
            conv(R, 0, 2)
            regroup("x", 1)
            regroup("h", 1)
            quantise("x", 1)
            quantise("h", 1)
            for t in range(T):
                turn_weight(U, t)
            for t in range(T):
                copy_weight(U, t)
            quantise_weight(U, 0, 2)
            reset(0)
            quantise_weight(U, 2, 4)
            conv(R, 1, 2)
            for t in range(T):
                turn_weight(N, t)
            for t in range(T):
                copy_weight(N, t)
            quantise("hr", 0)
            regroup("x", 2)
            quantise_weight(N, 0, 2)
            quantise_weight(N, 2, 4)
            conv(U, 0, 3)
            for c in range(1, NCHUNK):
                if c > 1:
                    conv(R, c, 2)
                if 2 < c + 1 < NCHUNK:
                    regroup("x", c + 1)
                reset(c)
                keep_old(c - 1)
                if c + 1 < NCHUNK:
                    quantise("x", c + 1)
                conv(N, c - 1, 2)
                quantise("hr", c)
                make_diff(c - 1)
                if c + 1 < NCHUNK:
                    regroup("h", c + 1)
                scale_new(c - 1)
                if c + 1 < NCHUNK:
                    quantise("h", c + 1)
                scale_diff(c - 1)
                conv(U, c, 3)
                blend(c - 1, T)
            keep_old(NCHUNK - 1)
            conv(N, NCHUNK - 1, 2)
            make_diff(NCHUNK - 1)
            scale_new(NCHUNK - 1)
            scale_diff(NCHUNK - 1)
            blend(NCHUNK - 1, 2)
